import numpy as np
import ml_dtypes


def mxq(x, axis, fmt="e4m3"):
    dtype, down = {"e4m3": (ml_dtypes.float8_e4m3fn, 7), "e5m2": (ml_dtypes.float8_e5m2, 14)}[fmt]
    v = np.moveaxis(np.asarray(x, np.float32).astype(ml_dtypes.bfloat16).astype(np.float64), axis, -1)
    blocks = v.reshape(v.shape[:-1] + (-1, 32))
    amax = np.abs(blocks).max(-1, keepdims=True)
    byte = np.maximum(np.where(amax > 0, np.frexp(amax)[1] - 1 + 127, 0) - down, 1)
    scale = np.exp2(byte - 127.0)
    codes = (blocks / scale).astype(np.float32).astype(dtype).astype(np.float64)
    return np.moveaxis((codes * scale).reshape(v.shape), -1, axis)


WIDE = False


def mx_kscale(k):
    if not WIDE:
        return np.ones(k)
    levels = np.array([10, -10, 5, -5, 0])
    a = np.random.permutation(np.resize(levels, k // 512 * 4)).reshape(k // 512, 4)
    idx = np.arange(k)
    return np.exp2(a[idx // 512, idx % 128 // 32])


BF16 = ml_dtypes.bfloat16


def bf(x):
    return np.asarray(x, np.float32).astype(BF16)


def f64(x):
    return np.asarray(x).astype(np.float64)


E2M1 = np.array([0.0, 0.5, 1.0, 1.5, 2.0, 3.0, 4.0, 6.0, -0.0, -0.5, -1.0, -1.5, -2.0, -3.0, -4.0, -6.0])


def pack_weight(w, fmt):
    k, n = w.shape
    w = f64(bf(w)).reshape(k // 32, 32, n)
    amax = np.abs(w).max(1)
    if fmt == "e4m3":
        byte = np.frexp(amax)[1] - 1 + 127 - 7
    else:
        mant, ex = np.frexp(amax / 6.0)
        byte = np.where(mant > 0.5, ex, ex - 1) + 127
    byte = np.clip(np.where(amax > 0, byte, 1), 1, 254)
    scaled = (w * np.exp2(127.0 - byte)[:, None, :]).reshape(k, n).astype(np.float32)
    by_word = np.ascontiguousarray(scaled.reshape(k // 512, 128, 4, n).transpose(0, 1, 3, 2))
    if fmt == "e4m3":
        words = by_word.astype(ml_dtypes.float8_e4m3fn).view(np.uint8)
    else:
        c = by_word.astype(ml_dtypes.float4_e2m1fn).view(np.uint8) & 0xF
        words = c[..., 0::2] | (c[..., 1::2] << 4)
    return np.ascontiguousarray(words), np.ascontiguousarray(byte.astype(np.uint8).reshape(k // 512, 16, n))


def unpack_weight(words, scales, fmt):
    g, p, n, _ = words.shape
    if fmt == "e4m3":
        vals = np.ascontiguousarray(words).view(ml_dtypes.float8_e4m3fn).astype(np.float64)
    else:
        nib = np.empty((g, p, n, 4), np.uint8)
        nib[..., 0::2] = words & 0xF
        nib[..., 1::2] = words >> 4
        vals = E2M1[nib]
    vals = vals * np.repeat(np.exp2(scales.astype(np.float64) - 127.0), 8, axis=1)[..., None]
    return vals.transpose(0, 1, 3, 2).reshape(g * 512, n)

def pack4(w):
    words, scales = pack_weight(w, "e2m1")
    return words.reshape(words.shape[0], 128, -1), scales


def unpack4(words, scales):
    return unpack_weight(words.reshape(words.shape[0], 128, -1, 2), scales, "e2m1")


N, P, D, E, F = 4096, 3, 512, 128, 1024


def setup_inputs():
    s = mx_kscale(D)
    x = np.random.standard_normal((N, P, D)) + 0.5 * np.random.standard_normal((1, P, D))
    w1a_words, w1a_scales = pack4(np.random.standard_normal((D, E)) / np.sqrt(D) / s[:, None])
    w2a_words, w2a_scales = pack4(np.random.standard_normal((D, E)) / np.sqrt(D) / s[:, None])
    return {"x": bf(x * s),
            "w1a_words": w1a_words, "w1a_scales": w1a_scales,
            "w2a_words": w2a_words, "w2a_scales": w2a_scales}


def reference(x, w1a_words, w1a_scales, w2a_words, w2a_scales):
    h = f64(x)
    neigh = (h.sum(axis=1, keepdims=True) - h) * 0.5
    return (mxq(h, 2, "e4m3") @ unpack4(w2a_words, w2a_scales)) + (mxq(neigh, 2, "e4m3") @ unpack4(w1a_words, w1a_scales))

@@ -1,0 +1,163 @@
+from contextlib import ExitStack
+
+import concourse.mybir as mybir
+from concourse.masks import make_identity
+
+BF16 = mybir.dt.bfloat16
+F32 = mybir.dt.float32
+I32 = mybir.dt.int32
+U8 = mybir.dt.uint8
+U32 = mybir.dt.uint32
+FP8X4 = mybir.dt.float8_e4m3fn_x4
+FP4X4 = mybir.dt.float4_e2m1fn_x4
+
+ITEMS, HOPS, K, E = 4096, 3, 512, 128
+P = 128
+PACK = 4
+PLANES = 2
+SLOTS = ITEMS // P
+PAIR = 2
+STEP = 4
+STEPS = SLOTS // STEP
+PAIRS = SLOTS // PAIR
+COLS = STEP * P * PACK
+ROWS = STEP * P
+LEAD = 2
+LOADS_AHEAD = 8
+
+FLOPS = 2 * 2 * ITEMS * HOPS * K * E
+
+
+def tile_dogtaitujuanji_pa_t_kernel(
+    tc, x, w1a_words, w1a_scales, w2a_words, w2a_scales, out
+):
+    nc = tc.nc
+    x_rows = x.rearrange("(r t) h k -> r t h k", t=SLOTS)
+    out_rows = out.rearrange("(r t) h e -> r t h e", t=SLOTS)
+
+    with ExitStack() as ctx:
+        const = ctx.enter_context(tc.tile_pool(name="const", bufs=1))
+        x_pool = ctx.enter_context(tc.tile_pool(name="x_pool", bufs=LOADS_AHEAD))
+        lead_pool = ctx.enter_context(tc.tile_pool(name="lead_pool", bufs=LEAD + 1))
+        work = ctx.enter_context(tc.tile_pool(name="work", bufs=2))
+        turned_pool = ctx.enter_context(tc.psum_pool(name="turned_pool", bufs=5))
+        acc_pool = ctx.enter_context(tc.psum_pool(name="acc_pool", bufs=3))
+        ctx.enter_context(tc.manual_schedule())
+
+        loaded = {}
+
+        def load_pair(q):
+            x_sb = x_pool.tile([P, PAIR, HOPS, K], BF16, name="x_sb")
+            nc.sync.dma_start(out=x_sb[:], in_=x_rows[:, q * PAIR : (q + 1) * PAIR])
+            loaded[q] = x_sb
+
+        def load_weight(words, scales, codes, plane):
+            nc.sync.dma_start(out=codes.bitcast(I32), in_=words[0].bitcast(I32))
+            for r in range(4):
+                nc.sync.dma_start(
+                    out=plane[r:P:32, :].bitcast(I32), in_=scales[0, r:16:4, :].bitcast(I32)
+                )
+
+        identity = const.tile([P, P], F32, name="identity")
+        make_identity(nc, identity[:])
+        w_codes = const.tile([P, 2, 2 * E], U8, name="w_codes", align_bytes=64)
+        w_planes = const.tile([P, 2, E], U8, name="w_planes", align_bytes=64)
+        nc.vector.memset(w_planes[:].bitcast(I32), 0)
+
+        for q in range(STEP // PAIR * LEAD):
+            load_pair(q)
+        load_weight(w1a_words, w1a_scales, w_codes[:, 0, :], w_planes[:, 0, :])
+        load_weight(w2a_words, w2a_scales, w_codes[:, 1, :], w_planes[:, 1, :])
+        for q in range(STEP // PAIR * LEAD, LOADS_AHEAD):
+            load_pair(q)
+
+        grouped_of = {}
+        half0_of = {}
+
+        def turn(step):
+            grouped = lead_pool.tile([P, HOPS, COLS], BF16, name="grouped", align_bytes=64)
+            for part in range(STEP // PAIR):
+                q = step * (STEP // PAIR) + part
+                x_words = loaded.pop(q)[:].bitcast(F32)
+                for hop in range(HOPS):
+                    turned = turned_pool.tile([P, PAIR, PLANES, P], F32, name="turned")
+                    for t in range(PAIR):
+                        for u in range(PLANES):
+                            nc.tensor.transpose(
+                                turned[:, t, u, :],
+                                x_words[:, t, hop, u : K // 2 : PLANES],
+                                identity[:],
+                            )
+                    span = slice(part * PAIR * P * PACK, (part + 1) * PAIR * P * PACK)
+                    nc.scalar.copy(
+                        out=grouped[:, hop, span]
+                        .bitcast(F32)
+                        .rearrange("m (t r u) -> m t r u", t=PAIR, u=PLANES),
+                        in_=turned[:].rearrange("m t u r -> m t r u"),
+                    )
+                if q + LOADS_AHEAD < PAIRS:
+                    load_pair(q + LOADS_AHEAD)
+            half0 = lead_pool.tile([P, COLS], BF16, name="half0")
+            nc.scalar.mul(out=half0[:], in_=grouped[:, 0, :], mul=0.5)
+            grouped_of[step] = grouped
+            half0_of[step] = half0
+
+        def quantise(values, codes, scales):
+            for hop in range(HOPS):
+                nc.vector.quantize_mx(
+                    out=codes[:, hop, :].bitcast(FP8X4), scales=scales[:, hop, :], in_=values[:, hop, :]
+                )
+
+        def finish(step):
+            grouped = grouped_of.pop(step)
+            half0 = half0_of.pop(step)
+
+            half12 = work.tile([P, 2, COLS], BF16, name="half12")
+            nc.vector.tensor_scalar_mul(out=half12[:], in0=grouped[:, 1:3, :], scalar1=0.5)
+            x_codes = work.tile([P, HOPS, ROWS], U32, name="x_codes", align_bytes=64)
+            x_scales = work.tile([P, HOPS, ROWS], U8, name="x_scales", align_bytes=64)
+            quantise(grouped, x_codes, x_scales)
+
+            halves = [half0[:], half12[:, 0, :], half12[:, 1, :]]
+            neigh = work.tile([P, HOPS, COLS], BF16, name="neigh", align_bytes=64)
+            for hop in range(HOPS):
+                a, b = [h for h in range(HOPS) if h != hop]
+                nc.vector.tensor_tensor(
+                    out=neigh[:, hop, :], in0=halves[a], in1=halves[b], op=mybir.AluOpType.add
+                )
+            n_codes = work.tile([P, HOPS, ROWS], U32, name="n_codes", align_bytes=64)
+            n_scales = work.tile([P, HOPS, ROWS], U8, name="n_scales", align_bytes=64)
+            quantise(neigh, n_codes, n_scales)
+
+            result = work.tile([P, STEP, HOPS, E], F32, name="result")
+            for hop in range(HOPS):
+                acc = acc_pool.tile([P, STEP, E], F32, name="acc")
+                for t in range(STEP):
+                    rows = slice(t * P, (t + 1) * P)
+                    nc.tensor.matmul_mx(
+                        out=acc[:, t, :],
+                        lhsT=x_codes[:, hop, rows].bitcast(FP8X4),
+                        lhsT_scale=x_scales[:, hop, rows],
+                        rhs=w_codes[:, 1, :].bitcast(FP4X4),
+                        rhs_scale=w_planes[:, 1, :],
+                        start=True,
+                        stop=False,
+                    )
+                    nc.tensor.matmul_mx(
+                        out=acc[:, t, :],
+                        lhsT=n_codes[:, hop, rows].bitcast(FP8X4),
+                        lhsT_scale=n_scales[:, hop, rows],
+                        rhs=w_codes[:, 0, :].bitcast(FP4X4),
+                        rhs_scale=w_planes[:, 0, :],
+                        start=False,
+                        stop=True,
+                    )
+                nc.scalar.copy(out=result[:, :, hop, :], in_=acc[:])
+            nc.sync.dma_start(out=out_rows[:, step * STEP : (step + 1) * STEP], in_=result[:])
+
+        for step in range(LEAD):
+            turn(step)
+        for step in range(STEPS):
+            if step + LEAD < STEPS:
+                turn(step + LEAD)
+            finish(step)

@@ -16,13 +16,12 @@ P = 128
 PACK = 4
 PLANES = 2
 SLOTS = ITEMS // P
-PAIR = 2
-STEP = 4
+STEP = 2
 STEPS = SLOTS // STEP
-PAIRS = SLOTS // PAIR
-COLS = STEP * P * PACK
 ROWS = STEP * P
-LEAD = 2
+COLS = ROWS * PACK
+HOP_CUTS = ((0, 2), (2, 3))
+LEAD = 3
 LOADS_AHEAD = 8
 
 FLOPS = 2 * 2 * ITEMS * HOPS * K * E
@@ -40,16 +39,16 @@ def tile_dogtaitujuanji_pa_t_kernel(
         x_pool = ctx.enter_context(tc.tile_pool(name="x_pool", bufs=LOADS_AHEAD))
         lead_pool = ctx.enter_context(tc.tile_pool(name="lead_pool", bufs=LEAD + 1))
         work = ctx.enter_context(tc.tile_pool(name="work", bufs=2))
-        turned_pool = ctx.enter_context(tc.psum_pool(name="turned_pool", bufs=5))
-        acc_pool = ctx.enter_context(tc.psum_pool(name="acc_pool", bufs=3))
+        turned_pool = ctx.enter_context(tc.psum_pool(name="turned_pool", bufs=4))
+        acc_pool = ctx.enter_context(tc.psum_pool(name="acc_pool", bufs=2))
         ctx.enter_context(tc.manual_schedule())
 
         loaded = {}
 
-        def load_pair(q):
-            x_sb = x_pool.tile([P, PAIR, HOPS, K], BF16, name="x_sb")
-            nc.sync.dma_start(out=x_sb[:], in_=x_rows[:, q * PAIR : (q + 1) * PAIR])
-            loaded[q] = x_sb
+        def load(step):
+            x_sb = x_pool.tile([P, STEP, HOPS, K], BF16, name="x_sb")
+            nc.sync.dma_start(out=x_sb[:], in_=x_rows[:, step * STEP : (step + 1) * STEP])
+            loaded[step] = x_sb
 
         def load_weight(words, scales, codes, plane):
             nc.sync.dma_start(out=codes.bitcast(I32), in_=words[0].bitcast(I32))
@@ -64,95 +63,97 @@ def tile_dogtaitujuanji_pa_t_kernel(
         w_planes = const.tile([P, 2, E], U8, name="w_planes", align_bytes=64)
         nc.vector.memset(w_planes[:].bitcast(I32), 0)
 
-        for q in range(STEP // PAIR * LEAD):
-            load_pair(q)
+        for step in range(LEAD):
+            load(step)
         load_weight(w1a_words, w1a_scales, w_codes[:, 0, :], w_planes[:, 0, :])
         load_weight(w2a_words, w2a_scales, w_codes[:, 1, :], w_planes[:, 1, :])
-        for q in range(STEP // PAIR * LEAD, LOADS_AHEAD):
-            load_pair(q)
+        for step in range(LEAD, LOADS_AHEAD):
+            load(step)
 
         grouped_of = {}
         half0_of = {}
 
         def turn(step):
+            x_words = loaded.pop(step)[:].bitcast(F32)
             grouped = lead_pool.tile([P, HOPS, COLS], BF16, name="grouped", align_bytes=64)
-            for part in range(STEP // PAIR):
-                q = step * (STEP // PAIR) + part
-                x_words = loaded.pop(q)[:].bitcast(F32)
-                for hop in range(HOPS):
-                    turned = turned_pool.tile([P, PAIR, PLANES, P], F32, name="turned")
-                    for t in range(PAIR):
-                        for u in range(PLANES):
-                            nc.tensor.transpose(
-                                turned[:, t, u, :],
-                                x_words[:, t, hop, u : K // 2 : PLANES],
-                                identity[:],
-                            )
-                    span = slice(part * PAIR * P * PACK, (part + 1) * PAIR * P * PACK)
-                    nc.scalar.copy(
-                        out=grouped[:, hop, span]
-                        .bitcast(F32)
-                        .rearrange("m (t r u) -> m t r u", t=PAIR, u=PLANES),
-                        in_=turned[:].rearrange("m t u r -> m t r u"),
-                    )
-                if q + LOADS_AHEAD < PAIRS:
-                    load_pair(q + LOADS_AHEAD)
+            for hop in range(HOPS):
+                turned = turned_pool.tile([P, STEP, PLANES, P], F32, name="turned")
+                for t in range(STEP):
+                    for u in range(PLANES):
+                        nc.tensor.transpose(
+                            turned[:, t, u, :], x_words[:, t, hop, u : K // 2 : PLANES], identity[:]
+                        )
+                nc.scalar.copy(
+                    out=grouped[:, hop, :]
+                    .bitcast(F32)
+                    .rearrange("m (t r u) -> m t r u", t=STEP, u=PLANES),
+                    in_=turned[:].rearrange("m t u r -> m t r u"),
+                )
+            if step + LOADS_AHEAD < STEPS:
+                load(step + LOADS_AHEAD)
             half0 = lead_pool.tile([P, COLS], BF16, name="half0")
             nc.scalar.mul(out=half0[:], in_=grouped[:, 0, :], mul=0.5)
             grouped_of[step] = grouped
             half0_of[step] = half0
 
-        def quantise(values, codes, scales):
-            for hop in range(HOPS):
-                nc.vector.quantize_mx(
-                    out=codes[:, hop, :].bitcast(FP8X4), scales=scales[:, hop, :], in_=values[:, hop, :]
-                )
+        def quantise(values, codes, scales, cut):
+            first, end = cut
+            nc.vector.quantize_mx(
+                out=codes[:, first:end, :].rearrange("m h w -> m (h w)").bitcast(FP8X4),
+                scales=scales[:, first:end, :].rearrange("m h w -> m (h w)"),
+                in_=values[:, first:end, :].rearrange("m h c -> m (h c)"),
+            )
 
         def finish(step):
             grouped = grouped_of.pop(step)
             half0 = half0_of.pop(step)
-
-            half12 = work.tile([P, 2, COLS], BF16, name="half12")
-            nc.vector.tensor_scalar_mul(out=half12[:], in0=grouped[:, 1:3, :], scalar1=0.5)
             x_codes = work.tile([P, HOPS, ROWS], U32, name="x_codes", align_bytes=64)
             x_scales = work.tile([P, HOPS, ROWS], U8, name="x_scales", align_bytes=64)
-            quantise(grouped, x_codes, x_scales)
-
-            halves = [half0[:], half12[:, 0, :], half12[:, 1, :]]
+            n_codes = work.tile([P, HOPS, ROWS], U32, name="n_codes", align_bytes=64)
+            n_scales = work.tile([P, HOPS, ROWS], U8, name="n_scales", align_bytes=64)
+            half12 = work.tile([P, 2, COLS], BF16, name="half12")
             neigh = work.tile([P, HOPS, COLS], BF16, name="neigh", align_bytes=64)
+
+            quantise(grouped, x_codes, x_scales, HOP_CUTS[0])
+            nc.vector.tensor_scalar_mul(out=half12[:], in0=grouped[:, 1:3, :], scalar1=0.5)
+            quantise(grouped, x_codes, x_scales, HOP_CUTS[1])
+            halves = [half0[:], half12[:, 0, :], half12[:, 1, :]]
             for hop in range(HOPS):
                 a, b = [h for h in range(HOPS) if h != hop]
                 nc.vector.tensor_tensor(
                     out=neigh[:, hop, :], in0=halves[a], in1=halves[b], op=mybir.AluOpType.add
                 )
-            n_codes = work.tile([P, HOPS, ROWS], U32, name="n_codes", align_bytes=64)
-            n_scales = work.tile([P, HOPS, ROWS], U8, name="n_scales", align_bytes=64)
-            quantise(neigh, n_codes, n_scales)
+            for cut in HOP_CUTS:
+                quantise(neigh, n_codes, n_scales, cut)
 
+            acc = acc_pool.tile([P, HOPS, STEP, E], F32, name="acc")
             result = work.tile([P, STEP, HOPS, E], F32, name="result")
-            for hop in range(HOPS):
-                acc = acc_pool.tile([P, STEP, E], F32, name="acc")
-                for t in range(STEP):
-                    rows = slice(t * P, (t + 1) * P)
-                    nc.tensor.matmul_mx(
-                        out=acc[:, t, :],
-                        lhsT=x_codes[:, hop, rows].bitcast(FP8X4),
-                        lhsT_scale=x_scales[:, hop, rows],
-                        rhs=w_codes[:, 1, :].bitcast(FP4X4),
-                        rhs_scale=w_planes[:, 1, :],
-                        start=True,
-                        stop=False,
-                    )
-                    nc.tensor.matmul_mx(
-                        out=acc[:, t, :],
-                        lhsT=n_codes[:, hop, rows].bitcast(FP8X4),
-                        lhsT_scale=n_scales[:, hop, rows],
-                        rhs=w_codes[:, 0, :].bitcast(FP4X4),
-                        rhs_scale=w_planes[:, 0, :],
-                        start=False,
-                        stop=True,
-                    )
-                nc.scalar.copy(out=result[:, :, hop, :], in_=acc[:])
+            for first, end in HOP_CUTS:
+                for hop in range(first, end):
+                    for t in range(STEP):
+                        rows = slice(t * P, (t + 1) * P)
+                        nc.tensor.matmul_mx(
+                            out=acc[:, hop, t, :],
+                            lhsT=x_codes[:, hop, rows].bitcast(FP8X4),
+                            lhsT_scale=x_scales[:, hop, rows],
+                            rhs=w_codes[:, 1, :].bitcast(FP4X4),
+                            rhs_scale=w_planes[:, 1, :],
+                            start=True,
+                            stop=False,
+                        )
+                        nc.tensor.matmul_mx(
+                            out=acc[:, hop, t, :],
+                            lhsT=n_codes[:, hop, rows].bitcast(FP8X4),
+                            lhsT_scale=n_scales[:, hop, rows],
+                            rhs=w_codes[:, 0, :].bitcast(FP4X4),
+                            rhs_scale=w_planes[:, 0, :],
+                            start=False,
+                            stop=True,
+                        )
+                nc.scalar.copy(
+                    out=result[:, :, first:end, :].rearrange("r t h e -> r h t e"),
+                    in_=acc[:, first:end, :, :],
+                )
             nc.sync.dma_start(out=out_rows[:, step * STEP : (step + 1) * STEP], in_=result[:])
 
         for step in range(LEAD):

@@ -16,13 +16,13 @@ P = 128
 PACK = 4
 PLANES = 2
 SLOTS = ITEMS // P
-STEP = 2
+STEP = 4
+PAIR = 2
 STEPS = SLOTS // STEP
 ROWS = STEP * P
 COLS = ROWS * PACK
-HOP_CUTS = ((0, 2), (2, 3))
-LEAD = 3
-LOADS_AHEAD = 8
+LEAD = 2
+STEPS_LOADED = 4
 
 FLOPS = 2 * 2 * ITEMS * HOPS * K * E
 
@@ -36,19 +36,22 @@ def tile_dogtaitujuanji_pa_t_kernel(
 
     with ExitStack() as ctx:
         const = ctx.enter_context(tc.tile_pool(name="const", bufs=1))
-        x_pool = ctx.enter_context(tc.tile_pool(name="x_pool", bufs=LOADS_AHEAD))
+        x_pool = ctx.enter_context(tc.tile_pool(name="x_pool", bufs=STEPS_LOADED * HOPS))
         lead_pool = ctx.enter_context(tc.tile_pool(name="lead_pool", bufs=LEAD + 1))
         work = ctx.enter_context(tc.tile_pool(name="work", bufs=2))
-        turned_pool = ctx.enter_context(tc.psum_pool(name="turned_pool", bufs=4))
-        acc_pool = ctx.enter_context(tc.psum_pool(name="acc_pool", bufs=2))
+        result_pool = ctx.enter_context(tc.tile_pool(name="result_pool", bufs=2 * HOPS))
+        turned_pool = ctx.enter_context(tc.psum_pool(name="turned_pool", bufs=5))
+        acc_pool = ctx.enter_context(tc.psum_pool(name="acc_pool", bufs=3))
         ctx.enter_context(tc.manual_schedule())
 
         loaded = {}
 
         def load(step):
-            x_sb = x_pool.tile([P, STEP, HOPS, K], BF16, name="x_sb")
-            nc.sync.dma_start(out=x_sb[:], in_=x_rows[:, step * STEP : (step + 1) * STEP])
-            loaded[step] = x_sb
+            items = slice(step * STEP, (step + 1) * STEP)
+            for hop in range(HOPS):
+                x_sb = x_pool.tile([P, STEP, K], BF16, name="x_sb")
+                nc.sync.dma_start(out=x_sb[:], in_=x_rows[:, items, hop, :])
+                loaded[step, hop] = x_sb
 
         def load_weight(words, scales, codes, plane):
             nc.sync.dma_start(out=codes.bitcast(I32), in_=words[0].bitcast(I32))
@@ -67,41 +70,41 @@ def tile_dogtaitujuanji_pa_t_kernel(
             load(step)
         load_weight(w1a_words, w1a_scales, w_codes[:, 0, :], w_planes[:, 0, :])
         load_weight(w2a_words, w2a_scales, w_codes[:, 1, :], w_planes[:, 1, :])
-        for step in range(LEAD, LOADS_AHEAD):
+        for step in range(LEAD, STEPS_LOADED):
             load(step)
 
         grouped_of = {}
         half0_of = {}
 
         def turn(step):
-            x_words = loaded.pop(step)[:].bitcast(F32)
             grouped = lead_pool.tile([P, HOPS, COLS], BF16, name="grouped", align_bytes=64)
             for hop in range(HOPS):
-                turned = turned_pool.tile([P, STEP, PLANES, P], F32, name="turned")
-                for t in range(STEP):
-                    for u in range(PLANES):
-                        nc.tensor.transpose(
-                            turned[:, t, u, :], x_words[:, t, hop, u : K // 2 : PLANES], identity[:]
-                        )
-                nc.scalar.copy(
-                    out=grouped[:, hop, :]
-                    .bitcast(F32)
-                    .rearrange("m (t r u) -> m t r u", t=STEP, u=PLANES),
-                    in_=turned[:].rearrange("m t u r -> m t r u"),
-                )
-            if step + LOADS_AHEAD < STEPS:
-                load(step + LOADS_AHEAD)
+                x_words = loaded.pop((step, hop))[:].bitcast(F32)
+                for first in range(0, STEP, PAIR):
+                    turned = turned_pool.tile([P, PAIR, PLANES, P], F32, name="turned")
+                    for t in range(PAIR):
+                        for u in range(PLANES):
+                            nc.tensor.transpose(
+                                turned[:, t, u, :],
+                                x_words[:, first + t, u : K // 2 : PLANES],
+                                identity[:],
+                            )
+                    nc.scalar.copy(
+                        out=grouped[:, hop, first * P * PACK : (first + PAIR) * P * PACK]
+                        .bitcast(F32)
+                        .rearrange("m (t r u) -> m t r u", t=PAIR, u=PLANES),
+                        in_=turned[:].rearrange("m t u r -> m t r u"),
+                    )
+            if step + STEPS_LOADED < STEPS:
+                load(step + STEPS_LOADED)
             half0 = lead_pool.tile([P, COLS], BF16, name="half0")
             nc.scalar.mul(out=half0[:], in_=grouped[:, 0, :], mul=0.5)
             grouped_of[step] = grouped
             half0_of[step] = half0
 
-        def quantise(values, codes, scales, cut):
-            first, end = cut
+        def quantise(values, codes, scales, hop):
             nc.vector.quantize_mx(
-                out=codes[:, first:end, :].rearrange("m h w -> m (h w)").bitcast(FP8X4),
-                scales=scales[:, first:end, :].rearrange("m h w -> m (h w)"),
-                in_=values[:, first:end, :].rearrange("m h c -> m (h c)"),
+                out=codes[:, hop, :].bitcast(FP8X4), scales=scales[:, hop, :], in_=values[:, hop, :]
             )
 
         def finish(step):
@@ -114,47 +117,46 @@ def tile_dogtaitujuanji_pa_t_kernel(
             half12 = work.tile([P, 2, COLS], BF16, name="half12")
             neigh = work.tile([P, HOPS, COLS], BF16, name="neigh", align_bytes=64)
 
-            quantise(grouped, x_codes, x_scales, HOP_CUTS[0])
+            quantise(grouped, x_codes, x_scales, 0)
+            quantise(grouped, x_codes, x_scales, 1)
             nc.vector.tensor_scalar_mul(out=half12[:], in0=grouped[:, 1:3, :], scalar1=0.5)
-            quantise(grouped, x_codes, x_scales, HOP_CUTS[1])
+            quantise(grouped, x_codes, x_scales, 2)
             halves = [half0[:], half12[:, 0, :], half12[:, 1, :]]
             for hop in range(HOPS):
                 a, b = [h for h in range(HOPS) if h != hop]
                 nc.vector.tensor_tensor(
                     out=neigh[:, hop, :], in0=halves[a], in1=halves[b], op=mybir.AluOpType.add
                 )
-            for cut in HOP_CUTS:
-                quantise(neigh, n_codes, n_scales, cut)
+            for hop in range(HOPS):
+                quantise(neigh, n_codes, n_scales, hop)
 
-            acc = acc_pool.tile([P, HOPS, STEP, E], F32, name="acc")
-            result = work.tile([P, STEP, HOPS, E], F32, name="result")
-            for first, end in HOP_CUTS:
-                for hop in range(first, end):
-                    for t in range(STEP):
-                        rows = slice(t * P, (t + 1) * P)
-                        nc.tensor.matmul_mx(
-                            out=acc[:, hop, t, :],
-                            lhsT=x_codes[:, hop, rows].bitcast(FP8X4),
-                            lhsT_scale=x_scales[:, hop, rows],
-                            rhs=w_codes[:, 1, :].bitcast(FP4X4),
-                            rhs_scale=w_planes[:, 1, :],
-                            start=True,
-                            stop=False,
-                        )
-                        nc.tensor.matmul_mx(
-                            out=acc[:, hop, t, :],
-                            lhsT=n_codes[:, hop, rows].bitcast(FP8X4),
-                            lhsT_scale=n_scales[:, hop, rows],
-                            rhs=w_codes[:, 0, :].bitcast(FP4X4),
-                            rhs_scale=w_planes[:, 0, :],
-                            start=False,
-                            stop=True,
-                        )
-                nc.scalar.copy(
-                    out=result[:, :, first:end, :].rearrange("r t h e -> r h t e"),
-                    in_=acc[:, first:end, :, :],
+            for hop in range(HOPS):
+                acc = acc_pool.tile([P, STEP, E], F32, name="acc")
+                for t in range(STEP):
+                    rows = slice(t * P, (t + 1) * P)
+                    nc.tensor.matmul_mx(
+                        out=acc[:, t, :],
+                        lhsT=x_codes[:, hop, rows].bitcast(FP8X4),
+                        lhsT_scale=x_scales[:, hop, rows],
+                        rhs=w_codes[:, 1, :].bitcast(FP4X4),
+                        rhs_scale=w_planes[:, 1, :],
+                        start=True,
+                        stop=False,
+                    )
+                    nc.tensor.matmul_mx(
+                        out=acc[:, t, :],
+                        lhsT=n_codes[:, hop, rows].bitcast(FP8X4),
+                        lhsT_scale=n_scales[:, hop, rows],
+                        rhs=w_codes[:, 0, :].bitcast(FP4X4),
+                        rhs_scale=w_planes[:, 0, :],
+                        start=False,
+                        stop=True,
+                    )
+                result = result_pool.tile([P, STEP, E], F32, name="result")
+                nc.scalar.copy(out=result[:], in_=acc[:])
+                nc.sync.dma_start(
+                    out=out_rows[:, step * STEP : (step + 1) * STEP, hop, :], in_=result[:]
                 )
-            nc.sync.dma_start(out=out_rows[:, step * STEP : (step + 1) * STEP], in_=result[:])
 
         for step in range(LEAD):
             turn(step)

@@ -74,7 +74,6 @@ def tile_dogtaitujuanji_pa_t_kernel(
             load(step)
 
         grouped_of = {}
-        half0_of = {}
 
         def turn(step):
             grouped = lead_pool.tile([P, HOPS, COLS], BF16, name="grouped", align_bytes=64)
@@ -97,10 +96,7 @@ def tile_dogtaitujuanji_pa_t_kernel(
                     )
             if step + STEPS_LOADED < STEPS:
                 load(step + STEPS_LOADED)
-            half0 = lead_pool.tile([P, COLS], BF16, name="half0")
-            nc.scalar.mul(out=half0[:], in_=grouped[:, 0, :], mul=0.5)
             grouped_of[step] = grouped
-            half0_of[step] = half0
 
         def quantise(values, codes, scales, hop):
             nc.vector.quantize_mx(
@@ -109,23 +105,19 @@ def tile_dogtaitujuanji_pa_t_kernel(
 
         def finish(step):
             grouped = grouped_of.pop(step)
-            half0 = half0_of.pop(step)
             x_codes = work.tile([P, HOPS, ROWS], U32, name="x_codes", align_bytes=64)
             x_scales = work.tile([P, HOPS, ROWS], U8, name="x_scales", align_bytes=64)
             n_codes = work.tile([P, HOPS, ROWS], U32, name="n_codes", align_bytes=64)
             n_scales = work.tile([P, HOPS, ROWS], U8, name="n_scales", align_bytes=64)
-            half12 = work.tile([P, 2, COLS], BF16, name="half12")
             neigh = work.tile([P, HOPS, COLS], BF16, name="neigh", align_bytes=64)
 
             quantise(grouped, x_codes, x_scales, 0)
             quantise(grouped, x_codes, x_scales, 1)
-            nc.vector.tensor_scalar_mul(out=half12[:], in0=grouped[:, 1:3, :], scalar1=0.5)
             quantise(grouped, x_codes, x_scales, 2)
-            halves = [half0[:], half12[:, 0, :], half12[:, 1, :]]
             for hop in range(HOPS):
                 a, b = [h for h in range(HOPS) if h != hop]
                 nc.vector.tensor_tensor(
-                    out=neigh[:, hop, :], in0=halves[a], in1=halves[b], op=mybir.AluOpType.add
+                    out=neigh[:, hop, :], in0=grouped[:, a, :], in1=grouped[:, b, :], op=mybir.AluOpType.add
                 )
             for hop in range(HOPS):
                 quantise(neigh, n_codes, n_scales, hop)
@@ -134,15 +126,16 @@ def tile_dogtaitujuanji_pa_t_kernel(
                 acc = acc_pool.tile([P, STEP, E], F32, name="acc")
                 for t in range(STEP):
                     rows = slice(t * P, (t + 1) * P)
-                    nc.tensor.matmul_mx(
-                        out=acc[:, t, :],
-                        lhsT=x_codes[:, hop, rows].bitcast(FP8X4),
-                        lhsT_scale=x_scales[:, hop, rows],
-                        rhs=w_codes[:, 1, :].bitcast(FP4X4),
-                        rhs_scale=w_planes[:, 1, :],
-                        start=True,
-                        stop=False,
-                    )
+                    for first_pass in (True, False):
+                        nc.tensor.matmul_mx(
+                            out=acc[:, t, :],
+                            lhsT=x_codes[:, hop, rows].bitcast(FP8X4),
+                            lhsT_scale=x_scales[:, hop, rows],
+                            rhs=w_codes[:, 1, :].bitcast(FP4X4),
+                            rhs_scale=w_planes[:, 1, :],
+                            start=first_pass,
+                            stop=False,
+                        )
                     nc.tensor.matmul_mx(
                         out=acc[:, t, :],
                         lhsT=n_codes[:, hop, rows].bitcast(FP8X4),
@@ -153,7 +146,7 @@ def tile_dogtaitujuanji_pa_t_kernel(
                         stop=True,
                     )
                 result = result_pool.tile([P, STEP, E], F32, name="result")
-                nc.scalar.copy(out=result[:], in_=acc[:])
+                nc.scalar.mul(out=result[:], in_=acc[:], mul=0.5)
                 nc.sync.dma_start(
                     out=out_rows[:, step * STEP : (step + 1) * STEP, hop, :], in_=result[:]
                 )

@@ -16,15 +16,27 @@ P = 128
 PACK = 4
 PLANES = 2
 SLOTS = ITEMS // P
-STEP = 4
-PAIR = 2
-STEPS = SLOTS // STEP
-ROWS = STEP * P
-COLS = ROWS * PACK
+CHUNKS = (1, 2, 2, 4, 4, 4, 4, 4, 4, 2, 1)
+BIG = max(CHUNKS)
 LEAD = 2
-STEPS_LOADED = 4
+LAG = 1
+LOADS = (1, 2, 2, 4, 4, 4, 4, 4, 4, 3)
+FIRST_LOADS = 4
+AHEAD = 12
+PARTS = 1
+UNITS_A_BANK = 2
+GROUPS_A_BANK = 4
+HOP_AT = (0, 2, 1)
+PLACE_OF_X = (0, 2, 1)
+PLACE_OF_SUM = (1, 0, 2)
 
 FLOPS = 2 * 2 * ITEMS * HOPS * K * E
+
+assert sum(CHUNKS) == SLOTS and sum(LOADS) == SLOTS
+
+
+def split(calls, parts):
+    return [calls[len(calls) * i // parts : len(calls) * (i + 1) // parts] for i in range(parts)]
 
 
 def tile_dogtaitujuanji_pa_t_kernel(
@@ -32,29 +44,32 @@ def tile_dogtaitujuanji_pa_t_kernel(
 ):
     nc = tc.nc
     x_rows = x.rearrange("(r t) h k -> r t h k", t=SLOTS)
-    out_rows = out.rearrange("(r t) h e -> r t h e", t=SLOTS)
+    out_rows = out.rearrange("(r t) h e -> r (t h e)", t=SLOTS)
+    first_item = [sum(CHUNKS[:c]) for c in range(len(CHUNKS))]
 
     with ExitStack() as ctx:
         const = ctx.enter_context(tc.tile_pool(name="const", bufs=1))
-        x_pool = ctx.enter_context(tc.tile_pool(name="x_pool", bufs=STEPS_LOADED * HOPS))
         lead_pool = ctx.enter_context(tc.tile_pool(name="lead_pool", bufs=LEAD + 1))
         work = ctx.enter_context(tc.tile_pool(name="work", bufs=2))
-        result_pool = ctx.enter_context(tc.tile_pool(name="result_pool", bufs=2 * HOPS))
+        code_pool = ctx.enter_context(tc.tile_pool(name="code_pool", bufs=LAG + 2))
+        result_pool = ctx.enter_context(tc.tile_pool(name="result_pool", bufs=3))
         turned_pool = ctx.enter_context(tc.psum_pool(name="turned_pool", bufs=5))
         acc_pool = ctx.enter_context(tc.psum_pool(name="acc_pool", bufs=3))
         ctx.enter_context(tc.manual_schedule())
 
-        loaded = {}
+        x_sb = const.tile([P, SLOTS, HOPS, K], BF16, name="x_sb")
+        x_words = x_sb[:].bitcast(F32)
+        started = set()
 
-        def load(step):
-            items = slice(step * STEP, (step + 1) * STEP)
-            for hop in range(HOPS):
-                x_sb = x_pool.tile([P, STEP, K], BF16, name="x_sb")
-                nc.sync.dma_start(out=x_sb[:], in_=x_rows[:, items, hop, :])
-                loaded[step, hop] = x_sb
+        def load(i, queue):
+            items = slice(sum(LOADS[:i]), sum(LOADS[: i + 1]))
+            queue.dma_start(out=x_sb[:, items, :, :], in_=x_rows[:, items, :, :])
+            started.add(i)
 
-        def load_weight(words, scales, codes, plane):
+        def load_codes(words, codes):
             nc.sync.dma_start(out=codes.bitcast(I32), in_=words[0].bitcast(I32))
+
+        def load_scales(scales, plane):
             for r in range(4):
                 nc.sync.dma_start(
                     out=plane[r:P:32, :].bitcast(I32), in_=scales[0, r:16:4, :].bitcast(I32)
@@ -66,94 +81,146 @@ def tile_dogtaitujuanji_pa_t_kernel(
         w_planes = const.tile([P, 2, E], U8, name="w_planes", align_bytes=64)
         nc.vector.memset(w_planes[:].bitcast(I32), 0)
 
-        for step in range(LEAD):
-            load(step)
-        load_weight(w1a_words, w1a_scales, w_codes[:, 0, :], w_planes[:, 0, :])
-        load_weight(w2a_words, w2a_scales, w_codes[:, 1, :], w_planes[:, 1, :])
-        for step in range(LEAD, STEPS_LOADED):
-            load(step)
+        load_scales(w1a_scales, w_planes[:, 0, :])
+        for i in range(FIRST_LOADS):
+            load(i, nc.scalar)
+        load_scales(w2a_scales, w_planes[:, 1, :])
+        load_codes(w1a_words, w_codes[:, 0, :])
+        load_codes(w2a_words, w_codes[:, 1, :])
 
         grouped_of = {}
 
-        def turn(step):
-            grouped = lead_pool.tile([P, HOPS, COLS], BF16, name="grouped", align_bytes=64)
-            for hop in range(HOPS):
-                x_words = loaded.pop((step, hop))[:].bitcast(F32)
-                for first in range(0, STEP, PAIR):
-                    turned = turned_pool.tile([P, PAIR, PLANES, P], F32, name="turned")
-                    for t in range(PAIR):
-                        for u in range(PLANES):
-                            nc.tensor.transpose(
-                                turned[:, t, u, :],
-                                x_words[:, first + t, u : K // 2 : PLANES],
-                                identity[:],
-                            )
-                    nc.scalar.copy(
-                        out=grouped[:, hop, first * P * PACK : (first + PAIR) * P * PACK]
-                        .bitcast(F32)
-                        .rearrange("m (t r u) -> m t r u", t=PAIR, u=PLANES),
-                        in_=turned[:].rearrange("m t u r -> m t r u"),
-                    )
-            if step + STEPS_LOADED < STEPS:
-                load(step + STEPS_LOADED)
-            grouped_of[step] = grouped
+        def turn_calls(c):
+            n = CHUNKS[c]
+            grouped = lead_pool.tile([P, HOPS * BIG * P * PACK], BF16, name="grouped", align_bytes=64)
+            grouped_of[c] = grouped
 
-        def quantise(values, codes, scales, hop):
+            def turn_bank(first):
+                units = range(first, min(first + UNITS_A_BANK, HOPS * n))
+                turned = turned_pool.tile([P, UNITS_A_BANK, PLANES, P], F32, name="turned")
+                for i, unit in enumerate(units):
+                    place, t = divmod(unit, n)
+                    hop = HOP_AT[place]
+                    for u in range(PLANES):
+                        nc.tensor.transpose(
+                            turned[:, i, u, :],
+                            x_words[:, first_item[c] + t, hop, u : K // 2 : PLANES],
+                            identity[:],
+                        )
+                nc.scalar.copy(
+                    out=grouped[:, first * P * PACK : (first + len(units)) * P * PACK]
+                    .bitcast(F32)
+                    .rearrange("m (i r u) -> m i r u", i=len(units), u=PLANES),
+                    in_=turned[:, : len(units)].rearrange("m i u r -> m i r u"),
+                )
+
+            return [(turn_bank, first) for first in range(0, HOPS * n, UNITS_A_BANK)]
+
+        codes_of = {}
+
+        def quantise(values, codes, scales, first, stop):
             nc.vector.quantize_mx(
-                out=codes[:, hop, :].bitcast(FP8X4), scales=scales[:, hop, :], in_=values[:, hop, :]
+                out=codes[:, first // PACK : stop // PACK].bitcast(FP8X4),
+                scales=scales[:, first // PACK : stop // PACK],
+                in_=values[:, first:stop],
             )
 
-        def finish(step):
-            grouped = grouped_of.pop(step)
-            x_codes = work.tile([P, HOPS, ROWS], U32, name="x_codes", align_bytes=64)
-            x_scales = work.tile([P, HOPS, ROWS], U8, name="x_scales", align_bytes=64)
-            n_codes = work.tile([P, HOPS, ROWS], U32, name="n_codes", align_bytes=64)
-            n_scales = work.tile([P, HOPS, ROWS], U8, name="n_scales", align_bytes=64)
-            neigh = work.tile([P, HOPS, COLS], BF16, name="neigh", align_bytes=64)
+        def vector_work(c):
+            width = CHUNKS[c] * P * PACK
+            grouped = grouped_of.pop(c)
+            x_codes = code_pool.tile([P, HOPS * BIG * P], U32, name="x_codes", align_bytes=64)
+            x_scales = code_pool.tile([P, HOPS * BIG * P], U8, name="x_scales", align_bytes=64)
+            n_codes = code_pool.tile([P, HOPS * BIG * P], U32, name="n_codes", align_bytes=64)
+            n_scales = code_pool.tile([P, HOPS * BIG * P], U8, name="n_scales", align_bytes=64)
+            sums = work.tile([P, HOPS * BIG * P * PACK], BF16, name="sums", align_bytes=64)
+            quantise(grouped, x_codes, x_scales, 0, 2 * width)
+            quantise(grouped, x_codes, x_scales, 2 * width, 3 * width)
+            nc.vector.tensor_tensor(
+                out=sums[:, : 2 * width],
+                in0=grouped[:, : 2 * width],
+                in1=grouped[:, width : 3 * width],
+                op=mybir.AluOpType.add,
+            )
+            nc.vector.tensor_tensor(
+                out=sums[:, 2 * width : 3 * width],
+                in0=grouped[:, :width],
+                in1=grouped[:, 2 * width : 3 * width],
+                op=mybir.AluOpType.add,
+            )
+            quantise(sums, n_codes, n_scales, 0, 2 * width)
+            quantise(sums, n_codes, n_scales, 2 * width, 3 * width)
+            codes_of[c] = (x_codes, x_scales, n_codes, n_scales)
 
-            quantise(grouped, x_codes, x_scales, 0)
-            quantise(grouped, x_codes, x_scales, 1)
-            quantise(grouped, x_codes, x_scales, 2)
-            for hop in range(HOPS):
-                a, b = [h for h in range(HOPS) if h != hop]
-                nc.vector.tensor_tensor(
-                    out=neigh[:, hop, :], in0=grouped[:, a, :], in1=grouped[:, b, :], op=mybir.AluOpType.add
-                )
-            for hop in range(HOPS):
-                quantise(neigh, n_codes, n_scales, hop)
+        def product_calls(c):
+            n = CHUNKS[c]
+            x_codes, x_scales, n_codes, n_scales = codes_of.pop(c)
+            result = result_pool.tile([P, BIG * HOPS * E], F32, name="result")
+            piecemeal = c == len(CHUNKS) - 1
+            groups_a_call = 1 if piecemeal else GROUPS_A_BANK
 
-            for hop in range(HOPS):
-                acc = acc_pool.tile([P, STEP, E], F32, name="acc")
-                for t in range(STEP):
-                    rows = slice(t * P, (t + 1) * P)
+            def product_bank(first):
+                groups = range(first, min(first + groups_a_call, n * HOPS))
+                acc = acc_pool.tile([P, GROUPS_A_BANK * E], F32, name="acc")
+                for i, group in enumerate(groups):
+                    t, hop = divmod(group, HOPS)
+                    x_cols = slice((PLACE_OF_X[hop] * n + t) * P, (PLACE_OF_X[hop] * n + t + 1) * P)
+                    n_cols = slice(
+                        (PLACE_OF_SUM[hop] * n + t) * P, (PLACE_OF_SUM[hop] * n + t + 1) * P
+                    )
                     for first_pass in (True, False):
                         nc.tensor.matmul_mx(
-                            out=acc[:, t, :],
-                            lhsT=x_codes[:, hop, rows].bitcast(FP8X4),
-                            lhsT_scale=x_scales[:, hop, rows],
+                            out=acc[:, i * E : (i + 1) * E],
+                            lhsT=x_codes[:, x_cols].bitcast(FP8X4),
+                            lhsT_scale=x_scales[:, x_cols],
                             rhs=w_codes[:, 1, :].bitcast(FP4X4),
                             rhs_scale=w_planes[:, 1, :],
                             start=first_pass,
                             stop=False,
                         )
                     nc.tensor.matmul_mx(
-                        out=acc[:, t, :],
-                        lhsT=n_codes[:, hop, rows].bitcast(FP8X4),
-                        lhsT_scale=n_scales[:, hop, rows],
+                        out=acc[:, i * E : (i + 1) * E],
+                        lhsT=n_codes[:, n_cols].bitcast(FP8X4),
+                        lhsT_scale=n_scales[:, n_cols],
                         rhs=w_codes[:, 0, :].bitcast(FP4X4),
                         rhs_scale=w_planes[:, 0, :],
                         start=False,
                         stop=True,
                     )
-                result = result_pool.tile([P, STEP, E], F32, name="result")
-                nc.scalar.mul(out=result[:], in_=acc[:], mul=0.5)
-                nc.sync.dma_start(
-                    out=out_rows[:, step * STEP : (step + 1) * STEP, hop, :], in_=result[:]
+                nc.scalar.mul(
+                    out=result[:, first * E : (first + len(groups)) * E],
+                    in_=acc[:, : len(groups) * E],
+                    mul=0.5,
                 )
+                stop = first + len(groups)
+                if piecemeal or stop == n * HOPS:
+                    start = first if piecemeal else 0
+                    nc.sync.dma_start(
+                        out=out_rows[
+                            :, (first_item[c] * HOPS + start) * E : (first_item[c] * HOPS + stop) * E
+                        ],
+                        in_=result[:, start * E : stop * E],
+                    )
 
-        for step in range(LEAD):
-            turn(step)
-        for step in range(STEPS):
-            if step + LEAD < STEPS:
-                turn(step + LEAD)
-            finish(step)
+            return [(product_bank, first) for first in range(0, n * HOPS, groups_a_call)]
+
+        def run(calls):
+            for call, first in calls:
+                call(first)
+
+        def refill(c):
+            for i in range(len(LOADS)):
+                if i not in started and c < len(CHUNKS) and sum(LOADS[:i]) < first_item[c] + AHEAD:
+                    load(i, nc.sync)
+
+        for c in range(LEAD):
+            refill(c)
+            run(turn_calls(c))
+        for c in range(len(CHUNKS) + LAG):
+            if c < len(CHUNKS):
+                vector_work(c)
+            refill(c + LEAD)
+            turns = turn_calls(c + LEAD) if c + LEAD < len(CHUNKS) else []
+            products = product_calls(c - LAG) if c >= LAG else []
+            for some_turns, some_products in zip(split(turns, PARTS), split(products, PARTS)):
+                run(some_products)
+                run(some_turns)

@@ -21,8 +21,9 @@ BIG = max(CHUNKS)
 LEAD = 2
 LAG = 1
 LOADS = (1, 2, 2, 4, 4, 4, 4, 4, 4, 3)
-FIRST_LOADS = 4
+FIRST_LOADS = 3
 AHEAD = 12
+WARM_UP = 4
 PARTS = 1
 UNITS_A_BANK = 2
 GROUPS_A_BANK = 4
@@ -75,18 +76,33 @@ def tile_dogtaitujuanji_pa_t_kernel(
                     out=plane[r:P:32, :].bitcast(I32), in_=scales[0, r:16:4, :].bitcast(I32)
                 )
 
+        warm = const.tile([P, 2], F32, name="warm")
+        nc.vector.memset(warm[:, 0:1], 0.0)
+        nc.scalar.copy(out=warm[:, 1:2], in_=warm[:, 0:1])
+
         identity = const.tile([P, P], F32, name="identity")
         make_identity(nc, identity[:])
         w_codes = const.tile([P, 2, 2 * E], U8, name="w_codes", align_bytes=64)
         w_planes = const.tile([P, 2, E], U8, name="w_planes", align_bytes=64)
         nc.vector.memset(w_planes[:].bitcast(I32), 0)
 
-        load_scales(w1a_scales, w_planes[:, 0, :])
         for i in range(FIRST_LOADS):
-            load(i, nc.scalar)
+            load(i, nc.sync)
+        load_scales(w1a_scales, w_planes[:, 0, :])
+        load(FIRST_LOADS, nc.sync)
         load_scales(w2a_scales, w_planes[:, 1, :])
         load_codes(w1a_words, w_codes[:, 0, :])
         load_codes(w2a_words, w_codes[:, 1, :])
+
+        ones = const.tile([P, GROUPS_A_BANK * E], BF16, name="ones")
+        nc.vector.memset(ones[:], 1.0)
+
+        def idle_matmuls(count):
+            for i in range(count):
+                scrap = acc_pool.tile([P, GROUPS_A_BANK * E], F32, name="acc")
+                nc.tensor.matmul(out=scrap[:], lhsT=ones[:, :P], rhs=ones[:], start=True, stop=True)
+
+        idle_matmuls(WARM_UP)
 
         grouped_of = {}
 
@@ -94,9 +110,10 @@ def tile_dogtaitujuanji_pa_t_kernel(
             n = CHUNKS[c]
             grouped = lead_pool.tile([P, HOPS * BIG * P * PACK], BF16, name="grouped", align_bytes=64)
             grouped_of[c] = grouped
+            units_a_call = 1 if c == 0 else UNITS_A_BANK
 
             def turn_bank(first):
-                units = range(first, min(first + UNITS_A_BANK, HOPS * n))
+                units = range(first, min(first + units_a_call, HOPS * n))
                 turned = turned_pool.tile([P, UNITS_A_BANK, PLANES, P], F32, name="turned")
                 for i, unit in enumerate(units):
                     place, t = divmod(unit, n)
@@ -114,7 +131,7 @@ def tile_dogtaitujuanji_pa_t_kernel(
                     in_=turned[:, : len(units)].rearrange("m i u r -> m i r u"),
                 )
 
-            return [(turn_bank, first) for first in range(0, HOPS * n, UNITS_A_BANK)]
+            return [(turn_bank, first) for first in range(0, HOPS * n, units_a_call)]
 
         codes_of = {}
 
@@ -133,8 +150,8 @@ def tile_dogtaitujuanji_pa_t_kernel(
             n_codes = code_pool.tile([P, HOPS * BIG * P], U32, name="n_codes", align_bytes=64)
             n_scales = code_pool.tile([P, HOPS * BIG * P], U8, name="n_scales", align_bytes=64)
             sums = work.tile([P, HOPS * BIG * P * PACK], BF16, name="sums", align_bytes=64)
-            quantise(grouped, x_codes, x_scales, 0, 2 * width)
-            quantise(grouped, x_codes, x_scales, 2 * width, 3 * width)
+            quantise(grouped, x_codes, x_scales, 0, width)
+            quantise(grouped, x_codes, x_scales, width, 3 * width)
             nc.vector.tensor_tensor(
                 out=sums[:, : 2 * width],
                 in0=grouped[:, : 2 * width],

@@ -24,7 +24,7 @@ LOADS = (1, 2, 2, 4, 4, 4, 4, 4, 4, 3)
 FIRST_LOADS = 3
 AHEAD = 12
 WARM_UP = 4
-PARTS = 1
+PARTS = 3
 UNITS_A_BANK = 2
 GROUPS_A_BANK = 4
 HOP_AT = (0, 2, 1)

@@ -23,7 +23,6 @@ LAG = 1
 LOADS = (1, 2, 2, 4, 4, 4, 4, 4, 4, 3)
 FIRST_LOADS = 3
 AHEAD = 12
-WARM_UP = 4
 PARTS = 3
 UNITS_A_BANK = 2
 GROUPS_A_BANK = 4
@@ -34,6 +33,12 @@ PLACE_OF_SUM = (1, 0, 2)
 FLOPS = 2 * 2 * ITEMS * HOPS * K * E
 
 assert sum(CHUNKS) == SLOTS and sum(LOADS) == SLOTS
+
+LAST = len(CHUNKS) - 1
+
+
+def places_by_tensor(c):
+    return (0, 1, 2) if c == LAST else (2,) if c >= LAST - 2 else ()
 
 
 def split(calls, parts):
@@ -94,15 +99,8 @@ def tile_dogtaitujuanji_pa_t_kernel(
         load_codes(w1a_words, w_codes[:, 0, :])
         load_codes(w2a_words, w_codes[:, 1, :])
 
-        ones = const.tile([P, GROUPS_A_BANK * E], BF16, name="ones")
-        nc.vector.memset(ones[:], 1.0)
-
-        def idle_matmuls(count):
-            for i in range(count):
-                scrap = acc_pool.tile([P, GROUPS_A_BANK * E], F32, name="acc")
-                nc.tensor.matmul(out=scrap[:], lhsT=ones[:, :P], rhs=ones[:], start=True, stop=True)
-
-        idle_matmuls(WARM_UP)
+        identity_bf = const.tile([P, P], BF16, name="identity_bf")
+        make_identity(nc, identity_bf[:])
 
         grouped_of = {}
 
@@ -133,13 +131,46 @@ def tile_dogtaitujuanji_pa_t_kernel(
 
             return [(turn_bank, first) for first in range(0, HOPS * n, units_a_call)]
 
+        tensor_sums_of = {}
+
+        def sum_calls(c):
+            n = CHUNKS[c]
+            places = places_by_tensor(c)
+            sums = const.tile(
+                [P, len(places) * n * P * PACK], BF16, name="tensor_sums_%d" % c, align_bytes=64
+            )
+            tensor_sums_of[c] = sums
+
+            def sum_bank(unit):
+                i, t = divmod(unit, n)
+                others = [hop for hop in range(HOPS) if PLACE_OF_SUM[hop] != places[i]]
+                added = turned_pool.tile([P, PACK, P], F32, name="turned")
+                for j in range(PACK):
+                    for hop in others:
+                        nc.tensor.matmul(
+                            out=added[:, j, :],
+                            lhsT=x_sb[:, first_item[c] + t, hop, j:K:PACK],
+                            rhs=identity_bf[:],
+                            start=hop == others[0],
+                            stop=hop == others[1],
+                        )
+                nc.scalar.copy(
+                    out=sums[:, unit * P * PACK : (unit + 1) * P * PACK].rearrange(
+                        "m (r j) -> m r j", j=PACK
+                    ),
+                    in_=added[:].rearrange("m j r -> m r j"),
+                )
+
+            return [(sum_bank, unit) for unit in range(len(places) * n)]
+
         codes_of = {}
 
-        def quantise(values, codes, scales, first, stop):
+        def quantise(values, codes, scales, first, stop, values_first=None):
+            at = first if values_first is None else values_first
             nc.vector.quantize_mx(
                 out=codes[:, first // PACK : stop // PACK].bitcast(FP8X4),
                 scales=scales[:, first // PACK : stop // PACK],
-                in_=values[:, first:stop],
+                in_=values[:, at : at + stop - first],
             )
 
         def vector_work(c):
@@ -149,31 +180,39 @@ def tile_dogtaitujuanji_pa_t_kernel(
             x_scales = code_pool.tile([P, HOPS * BIG * P], U8, name="x_scales", align_bytes=64)
             n_codes = code_pool.tile([P, HOPS * BIG * P], U32, name="n_codes", align_bytes=64)
             n_scales = code_pool.tile([P, HOPS * BIG * P], U8, name="n_scales", align_bytes=64)
-            sums = work.tile([P, HOPS * BIG * P * PACK], BF16, name="sums", align_bytes=64)
             quantise(grouped, x_codes, x_scales, 0, width)
             quantise(grouped, x_codes, x_scales, width, 3 * width)
-            nc.vector.tensor_tensor(
-                out=sums[:, : 2 * width],
-                in0=grouped[:, : 2 * width],
-                in1=grouped[:, width : 3 * width],
-                op=mybir.AluOpType.add,
-            )
-            nc.vector.tensor_tensor(
-                out=sums[:, 2 * width : 3 * width],
-                in0=grouped[:, :width],
-                in1=grouped[:, 2 * width : 3 * width],
-                op=mybir.AluOpType.add,
-            )
+            by_tensor = places_by_tensor(c)
+            if len(by_tensor) < HOPS:
+                sums = work.tile([P, HOPS * BIG * P * PACK], BF16, name="sums", align_bytes=64)
+                nc.vector.tensor_tensor(
+                    out=sums[:, : 2 * width],
+                    in0=grouped[:, : 2 * width],
+                    in1=grouped[:, width : 3 * width],
+                    op=mybir.AluOpType.add,
+                )
+            if not by_tensor:
+                nc.vector.tensor_tensor(
+                    out=sums[:, 2 * width : 3 * width],
+                    in0=grouped[:, :width],
+                    in1=grouped[:, 2 * width : 3 * width],
+                    op=mybir.AluOpType.add,
+                )
+            if len(by_tensor) == HOPS:
+                sums = tensor_sums_of[c]
             quantise(sums, n_codes, n_scales, 0, 2 * width)
-            quantise(sums, n_codes, n_scales, 2 * width, 3 * width)
+            if len(by_tensor) == 1:
+                quantise(tensor_sums_of[c], n_codes, n_scales, 2 * width, 3 * width, values_first=0)
+            else:
+                quantise(sums, n_codes, n_scales, 2 * width, 3 * width)
             codes_of[c] = (x_codes, x_scales, n_codes, n_scales)
 
         def product_calls(c):
             n = CHUNKS[c]
             x_codes, x_scales, n_codes, n_scales = codes_of.pop(c)
             result = result_pool.tile([P, BIG * HOPS * E], F32, name="result")
-            piecemeal = c == len(CHUNKS) - 1
-            groups_a_call = 1 if piecemeal else GROUPS_A_BANK
+            piecemeal = c >= LAST - 2
+            groups_a_call = 1 if c == LAST else GROUPS_A_BANK
 
             def product_bank(first):
                 groups = range(first, min(first + groups_a_call, n * HOPS))
@@ -237,6 +276,9 @@ def tile_dogtaitujuanji_pa_t_kernel(
                 vector_work(c)
             refill(c + LEAD)
             turns = turn_calls(c + LEAD) if c + LEAD < len(CHUNKS) else []
+            for d in range(len(CHUNKS)):
+                if places_by_tensor(d) and min(d - 1, LAST - LEAD) == c:
+                    turns = turns + sum_calls(d)
             products = product_calls(c - LAG) if c >= LAG else []
             for some_turns, some_products in zip(split(turns, PARTS), split(products, PARTS)):
                 run(some_products)

@@ -37,8 +37,8 @@ assert sum(CHUNKS) == SLOTS and sum(LOADS) == SLOTS
 LAST = len(CHUNKS) - 1
 
 
-def places_by_tensor(c):
-    return (0, 1, 2) if c == LAST else (2,) if c >= LAST - 2 else ()
+def units_by_tensor(c):
+    return 1 if CHUNKS[c] > 1 else 0
 
 
 def split(calls, parts):
@@ -131,19 +131,16 @@ def tile_dogtaitujuanji_pa_t_kernel(
 
             return [(turn_bank, first) for first in range(0, HOPS * n, units_a_call)]
 
-        tensor_sums_of = {}
+        sums_of = {}
 
         def sum_calls(c):
             n = CHUNKS[c]
-            places = places_by_tensor(c)
-            sums = const.tile(
-                [P, len(places) * n * P * PACK], BF16, name="tensor_sums_%d" % c, align_bytes=64
-            )
-            tensor_sums_of[c] = sums
+            sums = work.tile([P, HOPS * BIG * P * PACK], BF16, name="sums", align_bytes=64)
+            sums_of[c] = sums
 
             def sum_bank(unit):
-                i, t = divmod(unit, n)
-                others = [hop for hop in range(HOPS) if PLACE_OF_SUM[hop] != places[i]]
+                place, t = divmod(unit, n)
+                others = [hop for hop in range(HOPS) if PLACE_OF_SUM[hop] != place]
                 added = turned_pool.tile([P, PACK, P], F32, name="turned")
                 for j in range(PACK):
                     for hop in others:
@@ -161,7 +158,7 @@ def tile_dogtaitujuanji_pa_t_kernel(
                     in_=added[:].rearrange("m j r -> m r j"),
                 )
 
-            return [(sum_bank, unit) for unit in range(len(places) * n)]
+            return [(sum_bank, unit) for unit in range(HOPS * n - units_by_tensor(c), HOPS * n)]
 
         codes_of = {}
 
@@ -182,29 +179,22 @@ def tile_dogtaitujuanji_pa_t_kernel(
             n_scales = code_pool.tile([P, HOPS * BIG * P], U8, name="n_scales", align_bytes=64)
             quantise(grouped, x_codes, x_scales, 0, width)
             quantise(grouped, x_codes, x_scales, width, 3 * width)
-            by_tensor = places_by_tensor(c)
-            if len(by_tensor) < HOPS:
-                sums = work.tile([P, HOPS * BIG * P * PACK], BF16, name="sums", align_bytes=64)
-                nc.vector.tensor_tensor(
-                    out=sums[:, : 2 * width],
-                    in0=grouped[:, : 2 * width],
-                    in1=grouped[:, width : 3 * width],
-                    op=mybir.AluOpType.add,
-                )
-            if not by_tensor:
-                nc.vector.tensor_tensor(
-                    out=sums[:, 2 * width : 3 * width],
-                    in0=grouped[:, :width],
-                    in1=grouped[:, 2 * width : 3 * width],
-                    op=mybir.AluOpType.add,
-                )
-            if len(by_tensor) == HOPS:
-                sums = tensor_sums_of[c]
+            sums = sums_of.pop(c)
+            nc.vector.tensor_tensor(
+                out=sums[:, : 2 * width],
+                in0=grouped[:, : 2 * width],
+                in1=grouped[:, width : 3 * width],
+                op=mybir.AluOpType.add,
+            )
+            mine = width - units_by_tensor(c) * P * PACK
+            nc.vector.tensor_tensor(
+                out=sums[:, 2 * width : 2 * width + mine],
+                in0=grouped[:, :mine],
+                in1=grouped[:, 2 * width : 2 * width + mine],
+                op=mybir.AluOpType.add,
+            )
             quantise(sums, n_codes, n_scales, 0, 2 * width)
-            if len(by_tensor) == 1:
-                quantise(tensor_sums_of[c], n_codes, n_scales, 2 * width, 3 * width, values_first=0)
-            else:
-                quantise(sums, n_codes, n_scales, 2 * width, 3 * width)
+            quantise(sums, n_codes, n_scales, 2 * width, 3 * width)
             codes_of[c] = (x_codes, x_scales, n_codes, n_scales)
 
         def product_calls(c):
@@ -271,14 +261,14 @@ def tile_dogtaitujuanji_pa_t_kernel(
         for c in range(LEAD):
             refill(c)
             run(turn_calls(c))
+        run(sum_calls(0))
         for c in range(len(CHUNKS) + LAG):
             if c < len(CHUNKS):
                 vector_work(c)
             refill(c + LEAD)
             turns = turn_calls(c + LEAD) if c + LEAD < len(CHUNKS) else []
-            for d in range(len(CHUNKS)):
-                if places_by_tensor(d) and min(d - 1, LAST - LEAD) == c:
-                    turns = turns + sum_calls(d)
+            if c + 1 < len(CHUNKS):
+                turns = sum_calls(c + 1) + turns
             products = product_calls(c - LAG) if c >= LAG else []
             for some_turns, some_products in zip(split(turns, PARTS), split(products, PARTS)):
                 run(some_products)

@@ -23,7 +23,7 @@ LAG = 1
 LOADS = (1, 2, 2, 4, 4, 4, 4, 4, 4, 3)
 FIRST_LOADS = 3
 AHEAD = 12
-PARTS = 3
+PARTS = 2
 UNITS_A_BANK = 2
 GROUPS_A_BANK = 4
 HOP_AT = (0, 2, 1)

@@ -20,8 +20,8 @@ CHUNKS = (1, 2, 2, 4, 4, 4, 4, 4, 4, 2, 1)
 BIG = max(CHUNKS)
 LEAD = 2
 LAG = 1
-LOADS = (1, 2, 2, 4, 4, 4, 4, 4, 4, 3)
-FIRST_LOADS = 3
+LOADS = (1, 1, 1, 2, 2, 2, 4, 4, 4, 4, 4, 3)
+FIRST_LOADS = 4
 AHEAD = 12
 PARTS = 2
 UNITS_A_BANK = 2
@@ -108,10 +108,16 @@ def tile_dogtaitujuanji_pa_t_kernel(
             n = CHUNKS[c]
             grouped = lead_pool.tile([P, HOPS * BIG * P * PACK], BF16, name="grouped", align_bytes=64)
             grouped_of[c] = grouped
+            grouped_units = (
+                grouped[:, : HOPS * n * P * PACK]
+                .bitcast(F32)
+                .rearrange("m (q r u) -> m q r u", q=HOPS * n, u=PLANES)
+            )
             units_a_call = 1 if c == 0 else UNITS_A_BANK
+            by_item = [place * n + t for t in range(n) for place in range(HOPS)]
 
             def turn_bank(first):
-                units = range(first, min(first + units_a_call, HOPS * n))
+                units = sorted(by_item[first : first + units_a_call])
                 turned = turned_pool.tile([P, UNITS_A_BANK, PLANES, P], F32, name="turned")
                 for i, unit in enumerate(units):
                     place, t = divmod(unit, n)
@@ -123,9 +129,7 @@ def tile_dogtaitujuanji_pa_t_kernel(
                             identity[:],
                         )
                 nc.scalar.copy(
-                    out=grouped[:, first * P * PACK : (first + len(units)) * P * PACK]
-                    .bitcast(F32)
-                    .rearrange("m (i r u) -> m i r u", i=len(units), u=PLANES),
+                    out=grouped_units[:, units[0] : units[-1] + 1 : max(units[-1] - units[0], 1)],
                     in_=turned[:, : len(units)].rearrange("m i u r -> m i r u"),
                 )
 

@@ -145,7 +145,7 @@ def tile_dogtaitujuanji_pa_t_kernel(
             def sum_bank(unit):
                 place, t = divmod(unit, n)
                 others = [hop for hop in range(HOPS) if PLACE_OF_SUM[hop] != place]
-                added = turned_pool.tile([P, PACK, P], F32, name="turned")
+                added = turned_pool.tile([P, PACK, P], BF16, name="turned")
                 for j in range(PACK):
                     for hop in others:
                         nc.tensor.matmul(

@@ -19,6 +19,7 @@ SLOTS = ITEMS // P
 CHUNKS = (1, 2, 2, 4, 4, 4, 4, 4, 4, 2, 1)
 BIG = max(CHUNKS)
 LEAD = 2
+KEPT_SLOTS = 2
 LAG = 1
 LOADS = (1, 1, 1, 2, 2, 2, 4, 4, 4, 4, 4, 3)
 FIRST_LOADS = 4
@@ -35,6 +36,18 @@ FLOPS = 2 * 2 * ITEMS * HOPS * K * E
 assert sum(CHUNKS) == SLOTS and sum(LOADS) == SLOTS
 
 LAST = len(CHUNKS) - 1
+
+
+def keeps(c):
+    return CHUNKS[c] >= KEPT_SLOTS
+
+
+def units_by_gpsimd(c):
+    return CHUNKS[c] // 2 if CHUNKS[c] > 1 else 0
+
+
+def gpsimd_adds(c):
+    return c >= 2
 
 
 def units_by_tensor(c):
@@ -59,7 +72,9 @@ def tile_dogtaitujuanji_pa_t_kernel(
         work = ctx.enter_context(tc.tile_pool(name="work", bufs=2))
         code_pool = ctx.enter_context(tc.tile_pool(name="code_pool", bufs=LAG + 2))
         result_pool = ctx.enter_context(tc.tile_pool(name="result_pool", bufs=3))
-        turned_pool = ctx.enter_context(tc.psum_pool(name="turned_pool", bufs=5))
+        single = ctx.enter_context(tc.tile_pool(name="single", bufs=1))
+        turned_pool = ctx.enter_context(tc.psum_pool(name="turned_pool", bufs=3))
+        kept_pool = ctx.enter_context(tc.psum_pool(name="kept_pool", bufs=2))
         acc_pool = ctx.enter_context(tc.psum_pool(name="acc_pool", bufs=3))
         ctx.enter_context(tc.manual_schedule())
 
@@ -103,6 +118,35 @@ def tile_dogtaitujuanji_pa_t_kernel(
         make_identity(nc, identity_bf[:])
 
         grouped_of = {}
+        kept_of = {}
+
+        def words_of(grouped, first, stop):
+            return grouped[:, first * P * PACK : stop * P * PACK].bitcast(F32)
+
+        def keep_calls(c):
+            n = CHUNKS[c]
+            if not keeps(c):
+                return []
+            kept_of[c] = {}
+
+            def keep_bank(t0):
+                kept = kept_pool.tile([P, PLANES, KEPT_SLOTS * P], F32, name="kept")
+                kept_of[c][t0] = kept
+                for t in range(t0, t0 + KEPT_SLOTS):
+                    for u in range(PLANES):
+                        nc.tensor.transpose(
+                            kept[:, u, (t - t0) * P : (t - t0 + 1) * P],
+                            x_words[:, first_item[c] + t, 2, u : K // 2 : PLANES],
+                            identity[:],
+                        )
+                nc.scalar.copy(
+                    out=words_of(grouped_of[c], n + t0, n + t0 + KEPT_SLOTS).rearrange(
+                        "m (r u) -> m r u", u=PLANES
+                    ),
+                    in_=kept[:].rearrange("m u r -> m r u"),
+                )
+
+            return [(keep_bank, t0) for t0 in range(0, n, KEPT_SLOTS)]
 
         def turn_calls(c):
             n = CHUNKS[c]
@@ -114,7 +158,8 @@ def tile_dogtaitujuanji_pa_t_kernel(
                 .rearrange("m (q r u) -> m q r u", q=HOPS * n, u=PLANES)
             )
             units_a_call = 1 if c == 0 else UNITS_A_BANK
-            by_item = [place * n + t for t in range(n) for place in range(HOPS)]
+            places = (0, 2) if keeps(c) else range(HOPS)
+            by_item = [place * n + t for t in range(n) for place in places]
 
             def turn_bank(first):
                 units = sorted(by_item[first : first + units_a_call])
@@ -133,7 +178,7 @@ def tile_dogtaitujuanji_pa_t_kernel(
                     in_=turned[:, : len(units)].rearrange("m i u r -> m i r u"),
                 )
 
-            return [(turn_bank, first) for first in range(0, HOPS * n, units_a_call)]
+            return [(turn_bank, first) for first in range(0, len(by_item), units_a_call)]
 
         sums_of = {}
 
@@ -143,8 +188,8 @@ def tile_dogtaitujuanji_pa_t_kernel(
             sums_of[c] = sums
 
             def sum_bank(unit):
-                place, t = divmod(unit, n)
-                others = [hop for hop in range(HOPS) if PLACE_OF_SUM[hop] != place]
+                t = unit - 2 * n
+                others = (0, 1)
                 added = turned_pool.tile([P, PACK, P], BF16, name="turned")
                 for j in range(PACK):
                     for hop in others:
@@ -162,7 +207,8 @@ def tile_dogtaitujuanji_pa_t_kernel(
                     in_=added[:].rearrange("m j r -> m r j"),
                 )
 
-            return [(sum_bank, unit) for unit in range(HOPS * n - units_by_tensor(c), HOPS * n)]
+            last = HOPS * n - units_by_gpsimd(c)
+            return [(sum_bank, unit) for unit in range(last - units_by_tensor(c), last)]
 
         codes_of = {}
 
@@ -181,24 +227,65 @@ def tile_dogtaitujuanji_pa_t_kernel(
             x_scales = code_pool.tile([P, HOPS * BIG * P], U8, name="x_scales", align_bytes=64)
             n_codes = code_pool.tile([P, HOPS * BIG * P], U32, name="n_codes", align_bytes=64)
             n_scales = code_pool.tile([P, HOPS * BIG * P], U8, name="n_scales", align_bytes=64)
-            quantise(grouped, x_codes, x_scales, 0, width)
-            quantise(grouped, x_codes, x_scales, width, 3 * width)
+            n = CHUNKS[c]
             sums = sums_of.pop(c)
-            nc.vector.tensor_tensor(
-                out=sums[:, : 2 * width],
-                in0=grouped[:, : 2 * width],
-                in1=grouped[:, width : 3 * width],
-                op=mybir.AluOpType.add,
-            )
-            mine = width - units_by_tensor(c) * P * PACK
-            nc.vector.tensor_tensor(
-                out=sums[:, 2 * width : 2 * width + mine],
-                in0=grouped[:, :mine],
-                in1=grouped[:, 2 * width : 2 * width + mine],
-                op=mybir.AluOpType.add,
-            )
+            unit = P * PACK
+            by_gpsimd = units_by_gpsimd(c)
+            theirs = n - by_gpsimd
+            mine = theirs - units_by_tensor(c)
+
+            def quantise_rows():
+                quantise(grouped, x_codes, x_scales, 0, width)
+                quantise(grouped, x_codes, x_scales, width, 3 * width)
+
+            def add(engine, out, first, stop):
+                engine.tensor_tensor(
+                    out=out,
+                    in0=grouped[:, first * unit : stop * unit],
+                    in1=grouped[:, 2 * width + first * unit : 2 * width + stop * unit],
+                    op=mybir.AluOpType.add,
+                )
+
+            if gpsimd_adds(c) is False:
+                quantise_rows()
+            if by_gpsimd:
+                gp_sums = single.tile([P, BIG // 2 * P * PACK], BF16, name="gp_sums", align_bytes=64)
+                if gpsimd_adds(c):
+                    add(nc.gpsimd, gp_sums[:, : by_gpsimd * unit], theirs, n)
+            if keeps(c):
+                for t0, kept in kept_of.pop(c).items():
+                    for place in range(2):
+                        hop_at = 2 * place * width + t0 * unit
+                        at = place * width + t0 * unit
+                        nc.vector.tensor_tensor(
+                            out=sums[:, at : at + KEPT_SLOTS * unit].rearrange(
+                                "m (r u e) -> m r u e", u=PLANES, e=2
+                            ),
+                            in0=kept[:].bitcast(BF16).rearrange("m u (r e) -> m r u e", e=2),
+                            in1=grouped[:, hop_at : hop_at + KEPT_SLOTS * unit].rearrange(
+                                "m (r u e) -> m r u e", u=PLANES, e=2
+                            ),
+                            op=mybir.AluOpType.add,
+                        )
+            else:
+                nc.vector.tensor_tensor(
+                    out=sums[:, : 2 * width],
+                    in0=grouped[:, : 2 * width],
+                    in1=grouped[:, width : 3 * width],
+                    op=mybir.AluOpType.add,
+                )
+            if gpsimd_adds(c):
+                quantise_rows()
+            if by_gpsimd and not gpsimd_adds(c):
+                add(nc.vector, gp_sums[:, : by_gpsimd * unit], theirs, n)
+            if mine:
+                add(nc.vector, sums[:, 2 * width : 2 * width + mine * unit], 0, mine)
             quantise(sums, n_codes, n_scales, 0, 2 * width)
-            quantise(sums, n_codes, n_scales, 2 * width, 3 * width)
+            if by_gpsimd:
+                quantise(
+                    gp_sums, n_codes, n_scales, 3 * width - by_gpsimd * unit, 3 * width, values_first=0
+                )
+            quantise(sums, n_codes, n_scales, 2 * width, 3 * width - by_gpsimd * unit)
             codes_of[c] = (x_codes, x_scales, n_codes, n_scales)
 
         def product_calls(c):
@@ -271,9 +358,15 @@ def tile_dogtaitujuanji_pa_t_kernel(
                 vector_work(c)
             refill(c + LEAD)
             turns = turn_calls(c + LEAD) if c + LEAD < len(CHUNKS) else []
+            kept = []
             if c + 1 < len(CHUNKS):
                 turns = sum_calls(c + 1) + turns
+                kept = keep_calls(c + 1)
             products = product_calls(c - LAG) if c >= LAG else []
-            for some_turns, some_products in zip(split(turns, PARTS), split(products, PARTS)):
+            for part, (some_turns, some_products) in enumerate(
+                zip(split(turns, PARTS), split(products, PARTS))
+            ):
                 run(some_products)
+                if part == 0:
+                    run(kept)
                 run(some_turns)

@@ -24,7 +24,7 @@ LAG = 1
 LOADS = (1, 1, 1, 2, 2, 2, 4, 4, 4, 4, 4, 3)
 FIRST_LOADS = 4
 AHEAD = 12
-PARTS = 2
+PARTS = 3
 UNITS_A_BANK = 2
 GROUPS_A_BANK = 4
 HOP_AT = (0, 2, 1)

@@ -27,13 +27,15 @@ AHEAD = 12
 PARTS = 3
 UNITS_A_BANK = 2
 GROUPS_A_BANK = 4
-HOP_AT = (0, 2, 1)
-PLACE_OF_X = (0, 2, 1)
-PLACE_OF_SUM = (1, 0, 2)
+ROW_PLACES, SUM_PLACES = 4, 2
+SUM_01 = 3
+PLACE_OF_SUM = (5, 4, SUM_01)
 
 FLOPS = 2 * 2 * ITEMS * HOPS * K * E
 
 assert sum(CHUNKS) == SLOTS and sum(LOADS) == SLOTS
+
+FIRST_BY_GPSIMD = 2
 
 LAST = len(CHUNKS) - 1
 
@@ -43,15 +45,15 @@ def keeps(c):
 
 
 def units_by_gpsimd(c):
-    return CHUNKS[c] // 2 if CHUNKS[c] > 1 else 0
+    return CHUNKS[c] // 2 if gpsimd_adds(c) else 0
 
 
 def gpsimd_adds(c):
-    return c >= 2
+    return c >= FIRST_BY_GPSIMD and keeps(c)
 
 
 def units_by_tensor(c):
-    return 1 if CHUNKS[c] > 1 else 0
+    return 1 if CHUNKS[c] == BIG else 0
 
 
 def split(calls, parts):
@@ -72,7 +74,6 @@ def tile_dogtaitujuanji_pa_t_kernel(
         work = ctx.enter_context(tc.tile_pool(name="work", bufs=2))
         code_pool = ctx.enter_context(tc.tile_pool(name="code_pool", bufs=LAG + 2))
         result_pool = ctx.enter_context(tc.tile_pool(name="result_pool", bufs=3))
-        single = ctx.enter_context(tc.tile_pool(name="single", bufs=1))
         turned_pool = ctx.enter_context(tc.psum_pool(name="turned_pool", bufs=3))
         kept_pool = ctx.enter_context(tc.psum_pool(name="kept_pool", bufs=2))
         acc_pool = ctx.enter_context(tc.psum_pool(name="acc_pool", bufs=3))
@@ -140,7 +141,7 @@ def tile_dogtaitujuanji_pa_t_kernel(
                             identity[:],
                         )
                 nc.scalar.copy(
-                    out=words_of(grouped_of[c], n + t0, n + t0 + KEPT_SLOTS).rearrange(
+                    out=words_of(grouped_of[c], 2 * n + t0, 2 * n + t0 + KEPT_SLOTS).rearrange(
                         "m (r u) -> m r u", u=PLANES
                     ),
                     in_=kept[:].rearrange("m u r -> m r u"),
@@ -150,23 +151,22 @@ def tile_dogtaitujuanji_pa_t_kernel(
 
         def turn_calls(c):
             n = CHUNKS[c]
-            grouped = lead_pool.tile([P, HOPS * BIG * P * PACK], BF16, name="grouped", align_bytes=64)
+            grouped = lead_pool.tile([P, ROW_PLACES * BIG * P * PACK], BF16, name="grouped", align_bytes=64)
             grouped_of[c] = grouped
             grouped_units = (
-                grouped[:, : HOPS * n * P * PACK]
+                grouped[:, : ROW_PLACES * n * P * PACK]
                 .bitcast(F32)
-                .rearrange("m (q r u) -> m q r u", q=HOPS * n, u=PLANES)
+                .rearrange("m (q r u) -> m q r u", q=ROW_PLACES * n, u=PLANES)
             )
             units_a_call = 1 if c == 0 else UNITS_A_BANK
-            places = (0, 2) if keeps(c) else range(HOPS)
-            by_item = [place * n + t for t in range(n) for place in places]
+            hops = (0, 1) if keeps(c) else range(HOPS)
+            by_item = [hop * n + t for t in range(n) for hop in hops]
 
             def turn_bank(first):
                 units = sorted(by_item[first : first + units_a_call])
                 turned = turned_pool.tile([P, UNITS_A_BANK, PLANES, P], F32, name="turned")
                 for i, unit in enumerate(units):
-                    place, t = divmod(unit, n)
-                    hop = HOP_AT[place]
+                    hop, t = divmod(unit, n)
                     for u in range(PLANES):
                         nc.tensor.transpose(
                             turned[:, i, u, :],
@@ -184,11 +184,11 @@ def tile_dogtaitujuanji_pa_t_kernel(
 
         def sum_calls(c):
             n = CHUNKS[c]
-            sums = work.tile([P, HOPS * BIG * P * PACK], BF16, name="sums", align_bytes=64)
-            sums_of[c] = sums
+            sums_of[c] = work.tile([P, SUM_PLACES * BIG * P * PACK], BF16, name="sums", align_bytes=64)
+            grouped = grouped_of[c]
 
             def sum_bank(unit):
-                t = unit - 2 * n
+                t = unit - SUM_01 * n
                 others = (0, 1)
                 added = turned_pool.tile([P, PACK, P], BF16, name="turned")
                 for j in range(PACK):
@@ -201,96 +201,94 @@ def tile_dogtaitujuanji_pa_t_kernel(
                             stop=hop == others[1],
                         )
                 nc.scalar.copy(
-                    out=sums[:, unit * P * PACK : (unit + 1) * P * PACK].rearrange(
+                    out=grouped[:, unit * P * PACK : (unit + 1) * P * PACK].rearrange(
                         "m (r j) -> m r j", j=PACK
                     ),
                     in_=added[:].rearrange("m j r -> m r j"),
                 )
 
-            last = HOPS * n - units_by_gpsimd(c)
+            last = (SUM_01 + 1) * n - units_by_gpsimd(c)
             return [(sum_bank, unit) for unit in range(last - units_by_tensor(c), last)]
 
         codes_of = {}
 
-        def quantise(values, codes, scales, first, stop, values_first=None):
-            at = first if values_first is None else values_first
+        def quantise(c, values, place, stop, values_place=None):
+            codes, scales = codes_of[c]
+            n = CHUNKS[c] * P
+            at = (place if values_place is None else values_place) * n * PACK
             nc.vector.quantize_mx(
-                out=codes[:, first // PACK : stop // PACK].bitcast(FP8X4),
-                scales=scales[:, first // PACK : stop // PACK],
-                in_=values[:, at : at + stop - first],
+                out=codes[:, place * n : stop * n].bitcast(FP8X4),
+                scales=scales[:, place * n : stop * n],
+                in_=values[:, at : at + (stop - place) * n * PACK],
             )
 
         def vector_work(c):
-            width = CHUNKS[c] * P * PACK
-            grouped = grouped_of.pop(c)
-            x_codes = code_pool.tile([P, HOPS * BIG * P], U32, name="x_codes", align_bytes=64)
-            x_scales = code_pool.tile([P, HOPS * BIG * P], U8, name="x_scales", align_bytes=64)
-            n_codes = code_pool.tile([P, HOPS * BIG * P], U32, name="n_codes", align_bytes=64)
-            n_scales = code_pool.tile([P, HOPS * BIG * P], U8, name="n_scales", align_bytes=64)
             n = CHUNKS[c]
-            sums = sums_of.pop(c)
             unit = P * PACK
-            by_gpsimd = units_by_gpsimd(c)
-            theirs = n - by_gpsimd
+            width = n * unit
+            grouped = grouped_of.pop(c)
+            sums = sums_of.pop(c)
+            codes_of[c] = (
+                code_pool.tile([P, (ROW_PLACES + SUM_PLACES) * BIG * P], U32, name="codes", align_bytes=64),
+                code_pool.tile([P, (ROW_PLACES + SUM_PLACES) * BIG * P], U8, name="scales", align_bytes=64),
+            )
+            theirs = n - units_by_gpsimd(c)
             mine = theirs - units_by_tensor(c)
 
-            def quantise_rows():
-                quantise(grouped, x_codes, x_scales, 0, width)
-                quantise(grouped, x_codes, x_scales, width, 3 * width)
-
-            def add(engine, out, first, stop):
+            def add_01(engine, first, stop):
                 engine.tensor_tensor(
-                    out=out,
+                    out=grouped[:, SUM_01 * width + first * unit : SUM_01 * width + stop * unit],
                     in0=grouped[:, first * unit : stop * unit],
-                    in1=grouped[:, 2 * width + first * unit : 2 * width + stop * unit],
+                    in1=grouped[:, width + first * unit : width + stop * unit],
                     op=mybir.AluOpType.add,
                 )
 
-            if gpsimd_adds(c) is False:
-                quantise_rows()
-            if by_gpsimd:
-                gp_sums = single.tile([P, BIG // 2 * P * PACK], BF16, name="gp_sums", align_bytes=64)
-                if gpsimd_adds(c):
-                    add(nc.gpsimd, gp_sums[:, : by_gpsimd * unit], theirs, n)
-            if keeps(c):
+            def add_kept():
                 for t0, kept in kept_of.pop(c).items():
-                    for place in range(2):
-                        hop_at = 2 * place * width + t0 * unit
-                        at = place * width + t0 * unit
+                    for hop in range(2):
+                        slots = slice(hop * width + t0 * unit, hop * width + (t0 + KEPT_SLOTS) * unit)
                         nc.vector.tensor_tensor(
-                            out=sums[:, at : at + KEPT_SLOTS * unit].rearrange(
-                                "m (r u e) -> m r u e", u=PLANES, e=2
-                            ),
+                            out=sums[:, slots].rearrange("m (r u e) -> m r u e", u=PLANES, e=2),
                             in0=kept[:].bitcast(BF16).rearrange("m u (r e) -> m r u e", e=2),
-                            in1=grouped[:, hop_at : hop_at + KEPT_SLOTS * unit].rearrange(
-                                "m (r u e) -> m r u e", u=PLANES, e=2
-                            ),
+                            in1=grouped[:, slots].rearrange("m (r u e) -> m r u e", u=PLANES, e=2),
                             op=mybir.AluOpType.add,
                         )
+
+            if gpsimd_adds(c):
+                tick = work.tile([P, 1], U32, name="tick")
+                first_sum = ROW_PLACES * CHUNKS[c - 1] * P
+                nc.gpsimd.tensor_copy(
+                    out=tick[:], in_=codes_of[c - 1][0][:, first_sum : first_sum + 1]
+                )
+                add_01(nc.gpsimd, theirs, n)
+                add_kept()
+                quantise(c, grouped, 0, 2)
+                if mine:
+                    add_01(nc.vector, 0, mine)
+                quantise(c, sums, 4, 6, 0)
+                quantise(c, grouped, 2, 4)
+            elif keeps(c):
+                quantise(c, grouped, 0, 2)
+                add_kept()
+                add_01(nc.vector, 0, mine)
+                quantise(c, sums, 4, 6, 0)
+                quantise(c, grouped, 2, 4)
             else:
+                quantise(c, grouped, 0, 1)
+                quantise(c, grouped, 1, 3)
                 nc.vector.tensor_tensor(
-                    out=sums[:, : 2 * width],
-                    in0=grouped[:, : 2 * width],
-                    in1=grouped[:, width : 3 * width],
+                    out=sums[:, : 2 * width].rearrange("m (h v) -> m h v", h=2),
+                    in0=grouped[:, : 2 * width].rearrange("m (h v) -> m h v", h=2),
+                    in1=grouped[:, 2 * width : 3 * width].unsqueeze(1).to_broadcast([P, 2, width]),
                     op=mybir.AluOpType.add,
                 )
-            if gpsimd_adds(c):
-                quantise_rows()
-            if by_gpsimd and not gpsimd_adds(c):
-                add(nc.vector, gp_sums[:, : by_gpsimd * unit], theirs, n)
-            if mine:
-                add(nc.vector, sums[:, 2 * width : 2 * width + mine * unit], 0, mine)
-            quantise(sums, n_codes, n_scales, 0, 2 * width)
-            if by_gpsimd:
-                quantise(
-                    gp_sums, n_codes, n_scales, 3 * width - by_gpsimd * unit, 3 * width, values_first=0
-                )
-            quantise(sums, n_codes, n_scales, 2 * width, 3 * width - by_gpsimd * unit)
-            codes_of[c] = (x_codes, x_scales, n_codes, n_scales)
+                add_01(nc.vector, 0, mine)
+                quantise(c, sums, 4, 6, 0)
+                quantise(c, grouped, 3, 4)
 
         def product_calls(c):
             n = CHUNKS[c]
-            x_codes, x_scales, n_codes, n_scales = codes_of.pop(c)
+            codes, scales = codes_of.pop(c)
             result = result_pool.tile([P, BIG * HOPS * E], F32, name="result")
             piecemeal = c >= LAST - 2
             groups_a_call = 1 if c == LAST else GROUPS_A_BANK
@@ -300,15 +298,15 @@ def tile_dogtaitujuanji_pa_t_kernel(
                 acc = acc_pool.tile([P, GROUPS_A_BANK * E], F32, name="acc")
                 for i, group in enumerate(groups):
                     t, hop = divmod(group, HOPS)
-                    x_cols = slice((PLACE_OF_X[hop] * n + t) * P, (PLACE_OF_X[hop] * n + t + 1) * P)
+                    x_cols = slice((hop * n + t) * P, (hop * n + t + 1) * P)
                     n_cols = slice(
                         (PLACE_OF_SUM[hop] * n + t) * P, (PLACE_OF_SUM[hop] * n + t + 1) * P
                     )
                     for first_pass in (True, False):
                         nc.tensor.matmul_mx(
                             out=acc[:, i * E : (i + 1) * E],
-                            lhsT=x_codes[:, x_cols].bitcast(FP8X4),
-                            lhsT_scale=x_scales[:, x_cols],
+                            lhsT=codes[:, x_cols].bitcast(FP8X4),
+                            lhsT_scale=scales[:, x_cols],
                             rhs=w_codes[:, 1, :].bitcast(FP4X4),
                             rhs_scale=w_planes[:, 1, :],
                             start=first_pass,
@@ -316,8 +314,8 @@ def tile_dogtaitujuanji_pa_t_kernel(
                         )
                     nc.tensor.matmul_mx(
                         out=acc[:, i * E : (i + 1) * E],
-                        lhsT=n_codes[:, n_cols].bitcast(FP8X4),
-                        lhsT_scale=n_scales[:, n_cols],
+                        lhsT=codes[:, n_cols].bitcast(FP8X4),
+                        lhsT_scale=scales[:, n_cols],
                         rhs=w_codes[:, 0, :].bitcast(FP4X4),
                         rhs_scale=w_planes[:, 0, :],
                         start=False,

@@ -35,6 +35,7 @@ FLOPS = 2 * 2 * ITEMS * HOPS * K * E
 
 assert sum(CHUNKS) == SLOTS and sum(LOADS) == SLOTS
 
+GPSIMD_EIGHTHS = 3
 FIRST_BY_GPSIMD = 2
 
 LAST = len(CHUNKS) - 1
@@ -44,8 +45,8 @@ def keeps(c):
     return CHUNKS[c] >= KEPT_SLOTS
 
 
-def units_by_gpsimd(c):
-    return CHUNKS[c] // 2 if gpsimd_adds(c) else 0
+def rows_by_gpsimd(c):
+    return CHUNKS[c] * P * GPSIMD_EIGHTHS // 8 if gpsimd_adds(c) else 0
 
 
 def gpsimd_adds(c):
@@ -53,7 +54,7 @@ def gpsimd_adds(c):
 
 
 def units_by_tensor(c):
-    return 1 if CHUNKS[c] == BIG else 0
+    return 1 if CHUNKS[c] > 1 else 0
 
 
 def split(calls, parts):
@@ -207,8 +208,7 @@ def tile_dogtaitujuanji_pa_t_kernel(
                     in_=added[:].rearrange("m j r -> m r j"),
                 )
 
-            last = (SUM_01 + 1) * n - units_by_gpsimd(c)
-            return [(sum_bank, unit) for unit in range(last - units_by_tensor(c), last)]
+            return [(sum_bank, SUM_01 * n + t) for t in range(units_by_tensor(c))]
 
         codes_of = {}
 
@@ -232,14 +232,14 @@ def tile_dogtaitujuanji_pa_t_kernel(
                 code_pool.tile([P, (ROW_PLACES + SUM_PLACES) * BIG * P], U32, name="codes", align_bytes=64),
                 code_pool.tile([P, (ROW_PLACES + SUM_PLACES) * BIG * P], U8, name="scales", align_bytes=64),
             )
-            theirs = n - units_by_gpsimd(c)
-            mine = theirs - units_by_tensor(c)
+            mine = units_by_tensor(c) * unit
+            theirs = width - rows_by_gpsimd(c) * PACK
 
             def add_01(engine, first, stop):
                 engine.tensor_tensor(
-                    out=grouped[:, SUM_01 * width + first * unit : SUM_01 * width + stop * unit],
-                    in0=grouped[:, first * unit : stop * unit],
-                    in1=grouped[:, width + first * unit : width + stop * unit],
+                    out=grouped[:, SUM_01 * width + first : SUM_01 * width + stop],
+                    in0=grouped[:, first:stop],
+                    in1=grouped[:, width + first : width + stop],
                     op=mybir.AluOpType.add,
                 )
 
@@ -260,17 +260,17 @@ def tile_dogtaitujuanji_pa_t_kernel(
                 nc.gpsimd.tensor_copy(
                     out=tick[:], in_=codes_of[c - 1][0][:, first_sum : first_sum + 1]
                 )
-                add_01(nc.gpsimd, theirs, n)
+                add_01(nc.gpsimd, theirs, width)
                 add_kept()
                 quantise(c, grouped, 0, 2)
-                if mine:
-                    add_01(nc.vector, 0, mine)
+                if mine < theirs:
+                    add_01(nc.vector, mine, theirs)
                 quantise(c, sums, 4, 6, 0)
                 quantise(c, grouped, 2, 4)
             elif keeps(c):
                 quantise(c, grouped, 0, 2)
                 add_kept()
-                add_01(nc.vector, 0, mine)
+                add_01(nc.vector, mine, theirs)
                 quantise(c, sums, 4, 6, 0)
                 quantise(c, grouped, 2, 4)
             else:
@@ -282,7 +282,7 @@ def tile_dogtaitujuanji_pa_t_kernel(
                     in1=grouped[:, 2 * width : 3 * width].unsqueeze(1).to_broadcast([P, 2, width]),
                     op=mybir.AluOpType.add,
                 )
-                add_01(nc.vector, 0, mine)
+                add_01(nc.vector, mine, theirs)
                 quantise(c, sums, 4, 6, 0)
                 quantise(c, grouped, 3, 4)
 

@@ -54,7 +54,7 @@ def gpsimd_adds(c):
 
 
 def units_by_tensor(c):
-    return 1 if CHUNKS[c] > 1 else 0
+    return 1 if CHUNKS[c] == BIG else 0
 
 
 def split(calls, parts):
@@ -75,9 +75,9 @@ def tile_dogtaitujuanji_pa_t_kernel(
         work = ctx.enter_context(tc.tile_pool(name="work", bufs=2))
         code_pool = ctx.enter_context(tc.tile_pool(name="code_pool", bufs=LAG + 2))
         result_pool = ctx.enter_context(tc.tile_pool(name="result_pool", bufs=3))
-        turned_pool = ctx.enter_context(tc.psum_pool(name="turned_pool", bufs=3))
+        turned_pool = ctx.enter_context(tc.psum_pool(name="turned_pool", bufs=4))
         kept_pool = ctx.enter_context(tc.psum_pool(name="kept_pool", bufs=2))
-        acc_pool = ctx.enter_context(tc.psum_pool(name="acc_pool", bufs=3))
+        acc_pool = ctx.enter_context(tc.psum_pool(name="acc_pool", bufs=2))
         ctx.enter_context(tc.manual_schedule())
 
         x_sb = const.tile([P, SLOTS, HOPS, K], BF16, name="x_sb")
@@ -211,6 +211,15 @@ def tile_dogtaitujuanji_pa_t_kernel(
             return [(sum_bank, SUM_01 * n + t) for t in range(units_by_tensor(c))]
 
         codes_of = {}
+        late_banks = []
+
+        def next_bank(c):
+            if c >= LAST - 2:
+                late_banks.append(c)
+            if len(late_banks) % 2:
+                return turned_pool.tile([P, GROUPS_A_BANK * E], F32, name="turned")
+            return acc_pool.tile([P, GROUPS_A_BANK * E], F32, name="acc")
+
 
         def quantise(c, values, place, stop, values_place=None):
             codes, scales = codes_of[c]
@@ -249,8 +258,8 @@ def tile_dogtaitujuanji_pa_t_kernel(
                         slots = slice(hop * width + t0 * unit, hop * width + (t0 + KEPT_SLOTS) * unit)
                         nc.vector.tensor_tensor(
                             out=sums[:, slots].rearrange("m (r u e) -> m r u e", u=PLANES, e=2),
-                            in0=kept[:].bitcast(BF16).rearrange("m u (r e) -> m r u e", e=2),
-                            in1=grouped[:, slots].rearrange("m (r u e) -> m r u e", u=PLANES, e=2),
+                            in0=grouped[:, slots].rearrange("m (r u e) -> m r u e", u=PLANES, e=2),
+                            in1=kept[:].bitcast(BF16).rearrange("m u (r e) -> m r u e", e=2),
                             op=mybir.AluOpType.add,
                         )
 
@@ -295,7 +304,7 @@ def tile_dogtaitujuanji_pa_t_kernel(
 
             def product_bank(first):
                 groups = range(first, min(first + groups_a_call, n * HOPS))
-                acc = acc_pool.tile([P, GROUPS_A_BANK * E], F32, name="acc")
+                acc = next_bank(c)
                 for i, group in enumerate(groups):
                     t, hop = divmod(group, HOPS)
                     x_cols = slice((hop * n + t) * P, (hop * n + t + 1) * P)

from contextlib import ExitStack

import concourse.mybir as mybir
from concourse.masks import make_identity

BF16 = mybir.dt.bfloat16
F32 = mybir.dt.float32
I32 = mybir.dt.int32
U8 = mybir.dt.uint8
U32 = mybir.dt.uint32
FP8X4 = mybir.dt.float8_e4m3fn_x4
FP4X4 = mybir.dt.float4_e2m1fn_x4

ITEMS, HOPS, K, E = 4096, 3, 512, 128
P = 128
PACK = 4
PLANES = 2
SLOTS = ITEMS // P
CHUNKS = (1, 2, 2, 4, 4, 4, 4, 4, 4, 2, 1)
BIG = max(CHUNKS)
LEAD = 2
KEPT_SLOTS = 2
LAG = 1
LOADS = (1, 1, 1, 2, 2, 2, 4, 4, 4, 4, 4, 3)
FIRST_LOADS = 4
AHEAD = 12
PARTS = 3
UNITS_A_BANK = 2
GROUPS_A_BANK = 4
ROW_PLACES, SUM_PLACES = 4, 2
SUM_01 = 3
PLACE_OF_SUM = (5, 4, SUM_01)

FLOPS = 2 * 2 * ITEMS * HOPS * K * E

assert sum(CHUNKS) == SLOTS and sum(LOADS) == SLOTS

GPSIMD_EIGHTHS = 3
FIRST_BY_GPSIMD = 2

LAST = len(CHUNKS) - 1


def keeps(c):
    return CHUNKS[c] >= KEPT_SLOTS


def rows_by_gpsimd(c):
    return CHUNKS[c] * P * GPSIMD_EIGHTHS // 8 if gpsimd_adds(c) else 0


def gpsimd_adds(c):
    return c >= FIRST_BY_GPSIMD and keeps(c)


def units_by_tensor(c):
    return 1 if CHUNKS[c] == BIG else 0


def split(calls, parts):
    return [calls[len(calls) * i // parts : len(calls) * (i + 1) // parts] for i in range(parts)]


def tile_dogtaitujuanji_pa_t_kernel(
    tc, x, w1a_words, w1a_scales, w2a_words, w2a_scales, out
):
    nc = tc.nc
    x_rows = x.rearrange("(r t) h k -> r t h k", t=SLOTS)
    out_rows = out.rearrange("(r t) h e -> r (t h e)", t=SLOTS)
    first_item = [sum(CHUNKS[:c]) for c in range(len(CHUNKS))]

    with ExitStack() as ctx:
        const = ctx.enter_context(tc.tile_pool(name="const", bufs=1))
        lead_pool = ctx.enter_context(tc.tile_pool(name="lead_pool", bufs=LEAD + 1))
        work = ctx.enter_context(tc.tile_pool(name="work", bufs=2))
        code_pool = ctx.enter_context(tc.tile_pool(name="code_pool", bufs=LAG + 2))
        result_pool = ctx.enter_context(tc.tile_pool(name="result_pool", bufs=3))
        turned_pool = ctx.enter_context(tc.psum_pool(name="turned_pool", bufs=4))
        kept_pool = ctx.enter_context(tc.psum_pool(name="kept_pool", bufs=2))
        acc_pool = ctx.enter_context(tc.psum_pool(name="acc_pool", bufs=2))
        ctx.enter_context(tc.manual_schedule())

        x_sb = const.tile([P, SLOTS, HOPS, K], BF16, name="x_sb")
        x_words = x_sb[:].bitcast(F32)
        started = set()

        def load(i, queue):
            items = slice(sum(LOADS[:i]), sum(LOADS[: i + 1]))
            queue.dma_start(out=x_sb[:, items, :, :], in_=x_rows[:, items, :, :])
            started.add(i)

        def load_codes(words, codes):
            nc.sync.dma_start(out=codes.bitcast(I32), in_=words[0].bitcast(I32))

        def load_scales(scales, plane):
            for r in range(4):
                nc.sync.dma_start(
                    out=plane[r:P:32, :].bitcast(I32), in_=scales[0, r:16:4, :].bitcast(I32)
                )

        warm = const.tile([P, 2], F32, name="warm")
        nc.vector.memset(warm[:, 0:1], 0.0)
        nc.scalar.copy(out=warm[:, 1:2], in_=warm[:, 0:1])

        identity = const.tile([P, P], F32, name="identity")
        make_identity(nc, identity[:])
        w_codes = const.tile([P, 2, 2 * E], U8, name="w_codes", align_bytes=64)
        w_planes = const.tile([P, 2, E], U8, name="w_planes", align_bytes=64)
        nc.vector.memset(w_planes[:].bitcast(I32), 0)

        for i in range(FIRST_LOADS):
            load(i, nc.sync)
        load_scales(w1a_scales, w_planes[:, 0, :])
        load(FIRST_LOADS, nc.sync)
        load_scales(w2a_scales, w_planes[:, 1, :])
        load_codes(w1a_words, w_codes[:, 0, :])
        load_codes(w2a_words, w_codes[:, 1, :])

        identity_bf = const.tile([P, P], BF16, name="identity_bf")
        make_identity(nc, identity_bf[:])

        grouped_of = {}
        kept_of = {}

        def words_of(grouped, first, stop):
            return grouped[:, first * P * PACK : stop * P * PACK].bitcast(F32)

        def keep_calls(c):
            n = CHUNKS[c]
            if not keeps(c):
                return []
            kept_of[c] = {}

            def keep_bank(t0):
                kept = kept_pool.tile([P, PLANES, KEPT_SLOTS * P], F32, name="kept")
                kept_of[c][t0] = kept
                for t in range(t0, t0 + KEPT_SLOTS):
                    for u in range(PLANES):
                        nc.tensor.transpose(
                            kept[:, u, (t - t0) * P : (t - t0 + 1) * P],
                            x_words[:, first_item[c] + t, 2, u : K // 2 : PLANES],
                            identity[:],
                        )
                nc.scalar.copy(
                    out=words_of(grouped_of[c], 2 * n + t0, 2 * n + t0 + KEPT_SLOTS).rearrange(
                        "m (r u) -> m r u", u=PLANES
                    ),
                    in_=kept[:].rearrange("m u r -> m r u"),
                )

            return [(keep_bank, t0) for t0 in range(0, n, KEPT_SLOTS)]

        def turn_calls(c):
            n = CHUNKS[c]
            grouped = lead_pool.tile([P, ROW_PLACES * BIG * P * PACK], BF16, name="grouped", align_bytes=64)
            grouped_of[c] = grouped
            grouped_units = (
                grouped[:, : ROW_PLACES * n * P * PACK]
                .bitcast(F32)
                .rearrange("m (q r u) -> m q r u", q=ROW_PLACES * n, u=PLANES)
            )
            units_a_call = 1 if c == 0 else UNITS_A_BANK
            hops = (0, 1) if keeps(c) else range(HOPS)
            by_item = [hop * n + t for t in range(n) for hop in hops]

            def turn_bank(first):
                units = sorted(by_item[first : first + units_a_call])
                turned = turned_pool.tile([P, UNITS_A_BANK, PLANES, P], F32, name="turned")
                for i, unit in enumerate(units):
                    hop, t = divmod(unit, n)
                    for u in range(PLANES):
                        nc.tensor.transpose(
                            turned[:, i, u, :],
                            x_words[:, first_item[c] + t, hop, u : K // 2 : PLANES],
                            identity[:],
                        )
                nc.scalar.copy(
                    out=grouped_units[:, units[0] : units[-1] + 1 : max(units[-1] - units[0], 1)],
                    in_=turned[:, : len(units)].rearrange("m i u r -> m i r u"),
                )

            return [(turn_bank, first) for first in range(0, len(by_item), units_a_call)]

        sums_of = {}

        def sum_calls(c):
            n = CHUNKS[c]
            sums_of[c] = work.tile([P, SUM_PLACES * BIG * P * PACK], BF16, name="sums", align_bytes=64)
            grouped = grouped_of[c]

            def sum_bank(unit):
                t = unit - SUM_01 * n
                others = (0, 1)
                added = turned_pool.tile([P, PACK, P], BF16, name="turned")
                for j in range(PACK):
                    for hop in others:
                        nc.tensor.matmul(
                            out=added[:, j, :],
                            lhsT=x_sb[:, first_item[c] + t, hop, j:K:PACK],
                            rhs=identity_bf[:],
                            start=hop == others[0],
                            stop=hop == others[1],
                        )
                nc.scalar.copy(
                    out=grouped[:, unit * P * PACK : (unit + 1) * P * PACK].rearrange(
                        "m (r j) -> m r j", j=PACK
                    ),
                    in_=added[:].rearrange("m j r -> m r j"),
                )

            return [(sum_bank, SUM_01 * n + t) for t in range(units_by_tensor(c))]

        codes_of = {}
        late_banks = []

        def next_bank(c):
            if c >= LAST - 2:
                late_banks.append(c)
            if len(late_banks) % 2:
                return turned_pool.tile([P, GROUPS_A_BANK * E], F32, name="turned")
            return acc_pool.tile([P, GROUPS_A_BANK * E], F32, name="acc")


        def quantise(c, values, place, stop, values_place=None):
            codes, scales = codes_of[c]
            n = CHUNKS[c] * P
            at = (place if values_place is None else values_place) * n * PACK
            nc.vector.quantize_mx(
                out=codes[:, place * n : stop * n].bitcast(FP8X4),
                scales=scales[:, place * n : stop * n],
                in_=values[:, at : at + (stop - place) * n * PACK],
            )

        def vector_work(c):
            n = CHUNKS[c]
            unit = P * PACK
            width = n * unit
            grouped = grouped_of.pop(c)
            sums = sums_of.pop(c)
            codes_of[c] = (
                code_pool.tile([P, (ROW_PLACES + SUM_PLACES) * BIG * P], U32, name="codes", align_bytes=64),
                code_pool.tile([P, (ROW_PLACES + SUM_PLACES) * BIG * P], U8, name="scales", align_bytes=64),
            )
            mine = units_by_tensor(c) * unit
            theirs = width - rows_by_gpsimd(c) * PACK

            def add_01(engine, first, stop):
                engine.tensor_tensor(
                    out=grouped[:, SUM_01 * width + first : SUM_01 * width + stop],
                    in0=grouped[:, first:stop],
                    in1=grouped[:, width + first : width + stop],
                    op=mybir.AluOpType.add,
                )

            def add_kept():
                for t0, kept in kept_of.pop(c).items():
                    for hop in range(2):
                        slots = slice(hop * width + t0 * unit, hop * width + (t0 + KEPT_SLOTS) * unit)
                        nc.vector.tensor_tensor(
                            out=sums[:, slots].rearrange("m (r u e) -> m r u e", u=PLANES, e=2),
                            in0=grouped[:, slots].rearrange("m (r u e) -> m r u e", u=PLANES, e=2),
                            in1=kept[:].bitcast(BF16).rearrange("m u (r e) -> m r u e", e=2),
                            op=mybir.AluOpType.add,
                        )

            if gpsimd_adds(c):
                tick = work.tile([P, 1], U32, name="tick")
                first_sum = ROW_PLACES * CHUNKS[c - 1] * P
                nc.gpsimd.tensor_copy(
                    out=tick[:], in_=codes_of[c - 1][0][:, first_sum : first_sum + 1]
                )
                add_01(nc.gpsimd, theirs, width)
                add_kept()
                quantise(c, grouped, 0, 2)
                if mine < theirs:
                    add_01(nc.vector, mine, theirs)
                quantise(c, sums, 4, 6, 0)
                quantise(c, grouped, 2, 4)
            elif keeps(c):
                quantise(c, grouped, 0, 2)
                add_kept()
                add_01(nc.vector, mine, theirs)
                quantise(c, sums, 4, 6, 0)
                quantise(c, grouped, 2, 4)
            else:
                quantise(c, grouped, 0, 1)
                quantise(c, grouped, 1, 3)
                nc.vector.tensor_tensor(
                    out=sums[:, : 2 * width].rearrange("m (h v) -> m h v", h=2),
                    in0=grouped[:, : 2 * width].rearrange("m (h v) -> m h v", h=2),
                    in1=grouped[:, 2 * width : 3 * width].unsqueeze(1).to_broadcast([P, 2, width]),
                    op=mybir.AluOpType.add,
                )
                add_01(nc.vector, mine, theirs)
                quantise(c, sums, 4, 6, 0)
                quantise(c, grouped, 3, 4)

        def product_calls(c):
            n = CHUNKS[c]
            codes, scales = codes_of.pop(c)
            result = result_pool.tile([P, BIG * HOPS * E], F32, name="result")
            piecemeal = c >= LAST - 2
            groups_a_call = 1 if c == LAST else GROUPS_A_BANK

            def product_bank(first):
                groups = range(first, min(first + groups_a_call, n * HOPS))
                acc = next_bank(c)
                for i, group in enumerate(groups):
                    t, hop = divmod(group, HOPS)
                    x_cols = slice((hop * n + t) * P, (hop * n + t + 1) * P)
                    n_cols = slice(
                        (PLACE_OF_SUM[hop] * n + t) * P, (PLACE_OF_SUM[hop] * n + t + 1) * P
                    )
                    for first_pass in (True, False):
                        nc.tensor.matmul_mx(
                            out=acc[:, i * E : (i + 1) * E],
                            lhsT=codes[:, x_cols].bitcast(FP8X4),
                            lhsT_scale=scales[:, x_cols],
                            rhs=w_codes[:, 1, :].bitcast(FP4X4),
                            rhs_scale=w_planes[:, 1, :],
                            start=first_pass,
                            stop=False,
                        )
                    nc.tensor.matmul_mx(
                        out=acc[:, i * E : (i + 1) * E],
                        lhsT=codes[:, n_cols].bitcast(FP8X4),
                        lhsT_scale=scales[:, n_cols],
                        rhs=w_codes[:, 0, :].bitcast(FP4X4),
                        rhs_scale=w_planes[:, 0, :],
                        start=False,
                        stop=True,
                    )
                nc.scalar.mul(
                    out=result[:, first * E : (first + len(groups)) * E],
                    in_=acc[:, : len(groups) * E],
                    mul=0.5,
                )
                stop = first + len(groups)
                if piecemeal or stop == n * HOPS:
                    start = first if piecemeal else 0
                    nc.sync.dma_start(
                        out=out_rows[
                            :, (first_item[c] * HOPS + start) * E : (first_item[c] * HOPS + stop) * E
                        ],
                        in_=result[:, start * E : stop * E],
                    )

            return [(product_bank, first) for first in range(0, n * HOPS, groups_a_call)]

        def run(calls):
            for call, first in calls:
                call(first)

        def refill(c):
            for i in range(len(LOADS)):
                if i not in started and c < len(CHUNKS) and sum(LOADS[:i]) < first_item[c] + AHEAD:
                    load(i, nc.sync)

        for c in range(LEAD):
            refill(c)
            run(turn_calls(c))
        run(sum_calls(0))
        for c in range(len(CHUNKS) + LAG):
            if c < len(CHUNKS):
                vector_work(c)
            refill(c + LEAD)
            turns = turn_calls(c + LEAD) if c + LEAD < len(CHUNKS) else []
            kept = []
            if c + 1 < len(CHUNKS):
                turns = sum_calls(c + 1) + turns
                kept = keep_calls(c + 1)
            products = product_calls(c - LAG) if c >= LAG else []
            for part, (some_turns, some_products) in enumerate(
                zip(split(turns, PARTS), split(products, PARTS))
            ):
                run(some_products)
                if part == 0:
                    run(kept)
                run(some_turns)
